import numpy as np
import ml_dtypes


def mxq(x, axis, fmt="e4m3"):
    dtype, down = {"e4m3": (ml_dtypes.float8_e4m3fn, 7), "e5m2": (ml_dtypes.float8_e5m2, 14)}[fmt]
    v = np.moveaxis(np.asarray(x, np.float32).astype(ml_dtypes.bfloat16).astype(np.float64), axis, -1)
    blocks = v.reshape(v.shape[:-1] + (-1, 32))
    amax = np.abs(blocks).max(-1, keepdims=True)
    byte = np.maximum(np.where(amax > 0, np.frexp(amax)[1] - 1 + 127, 0) - down, 1)
    scale = np.exp2(byte - 127.0)
    codes = (blocks / scale).astype(np.float32).astype(dtype).astype(np.float64)
    return np.moveaxis((codes * scale).reshape(v.shape), -1, axis)


WIDE = False


def mx_kscale(k):
    if not WIDE:
        return np.ones(k)
    levels = np.array([10, -10, 5, -5, 0])
    a = np.random.permutation(np.resize(levels, k // 512 * 4)).reshape(k // 512, 4)
    idx = np.arange(k)
    return np.exp2(a[idx // 512, idx % 128 // 32])


BF16 = ml_dtypes.bfloat16


def bf(x):
    return np.asarray(x, np.float32).astype(BF16)


def f64(x):
    return np.asarray(x).astype(np.float64)


B, D_IN, D_H, C = 512, 1024, 4096, 128
TAU, T1, T2 = 0.5, 3, 3
G, GB = 3.0, 3.0


def inv_apprx(v, t, m):
    a = 2.0 - (2.0 / m) * v
    b = 1.0 - (2.0 / m) * v
    for _ in range(t):
        b = b * b
        a = a * (1.0 + b)
    return (2.0 / m) * a


def comp_max_tau(p, tau, t1, t2):
    res = np.concatenate([p, np.full((p.shape[0], 1), tau)], axis=1)
    for i in range(t1):
        res = res * res
        sum_res = res.sum(axis=1)
        m = (2.0 + tau * tau) if i == 0 else 2.0
        res = res * inv_apprx(sum_res, t2, m)[:, None]
    return res[:, -1]


def softmax(z):
    e = np.exp(z - z.max(-1, keepdims=True))
    return e / e.sum(-1, keepdims=True)


def mlp(xq, W1, b1, W2, b2):
    h = np.maximum((xq @ mxq(f64(W1), 0, "e4m3")) + f64(b1), 0.0)
    return softmax((mxq(h, 1, "e4m3") @ mxq(f64(W2), 0, "e4m3")) + f64(b2))


def setup_inputs():
    s, t = mx_kscale(D_IN), mx_kscale(D_H)
    return {"x": bf(np.random.standard_normal((B, D_IN)) * s),
            "W1o": bf(np.random.standard_normal((D_IN, D_H)) / np.sqrt(D_IN) / s[:, None] * t),
            "b1o": bf(np.random.standard_normal(D_H) * 0.2 * t),
            "W2o": bf(np.random.standard_normal((D_H, C)) * G / np.sqrt(D_H) / t[:, None]),
            "b2o": bf(np.random.standard_normal(C) * GB),
            "W1f": bf(np.random.standard_normal((D_IN, D_H)) / np.sqrt(D_IN) / s[:, None] * t),
            "b1f": bf(np.random.standard_normal(D_H) * 0.2 * t),
            "W2f": bf(np.random.standard_normal((D_H, C)) * G / np.sqrt(D_H) / t[:, None]),
            "b2f": bf(np.random.standard_normal(C) * GB)}


def reference(x, W1o, b1o, W2o, b2o, W1f, b1f, W2f, b2f):
    xq = mxq(f64(x), 1, "e4m3")
    x1 = mlp(xq, W1o, b1o, W2o, b2o)
    x2 = mlp(xq, W1f, b1f, W2f, b2f)
    cond_in = comp_max_tau(x1, TAU, T1, T2)
    return x1 * (1.0 - cond_in[:, None]) + x2 * cond_in[:, None]

@@ -1,0 +1,352 @@
+from contextlib import ExitStack
+
+import concourse.mybir as mybir
+from concourse.masks import make_identity
+
+F32 = mybir.dt.float32
+BF16 = mybir.dt.bfloat16
+U32 = mybir.dt.uint32
+U8 = mybir.dt.uint8
+FP8X4 = mybir.dt.float8_e4m3fn_x4
+ACT = mybir.ActivationFunctionType
+ALU = mybir.AluOpType
+AX = mybir.AxisListType
+
+P = 128
+PACK = 4
+K_PASS = P * PACK
+
+B, D_IN, D_H, C = 512, 1024, 4096, 128
+TAU, T1, T2 = 0.5, 3, 3
+NETS = 2
+IN_PASSES = D_IN // K_PASS
+ROUNDS = D_H // K_PASS
+TOTAL = NETS * ROUNDS
+B_TILES = B // P
+B1_ROWS = D_H // P
+B2_ROW = NETS * B1_ROWS
+RAW_BUFS = 6
+
+FLOPS = NETS * (2 * B * D_IN * D_H + 2 * B * D_H * C)
+
+
+def regroup(copy, grouped, planes):
+    copy(
+        out=grouped.rearrange("p (c i) j -> p c j i", i=4),
+        in_=planes.rearrange("p j (c i) -> p c j i", i=4),
+    )
+
+
+def tile_combnethe_pa_kernel(tc, x, W1o, b1o, W2o, b2o, W1f, b1f, W2f, b2f, out):
+    nc = tc.nc
+    W1, b1, W2, b2 = (W1o, W1f), (b1o, b1f), (W2o, W2f), (b2o, b2f)
+    with ExitStack() as ctx:
+        const = ctx.enter_context(tc.tile_pool(name="const", bufs=1))
+        w1_raw_pool = ctx.enter_context(tc.tile_pool(name="w1_raw", bufs=RAW_BUFS))
+        w1_grp_pool = ctx.enter_context(tc.tile_pool(name="w1_grp", bufs=3))
+        w1_mx_pool = ctx.enter_context(tc.tile_pool(name="w1_mx", bufs=3))
+        w2_stage = ctx.enter_context(tc.tile_pool(name="w2_stage", bufs=1))
+        w2_mx_pool = ctx.enter_context(tc.tile_pool(name="w2_mx", bufs=NETS))
+        h_pool = ctx.enter_context(tc.tile_pool(name="h", bufs=3))
+        soft = ctx.enter_context(tc.tile_pool(name="soft", bufs=1))
+        small = ctx.enter_context(tc.tile_pool(name="small", bufs=1))
+        psum_h = ctx.enter_context(tc.psum_pool(name="psum_h", bufs=4))
+        psum_l = ctx.enter_context(tc.psum_pool(name="psum_l", bufs=1))
+
+        w1_raw, w1_grp, w1_codes, w1_scales = {}, {}, {}, {}
+        w2_raw, w2_codes, w2_scales = {}, {}, {}
+        h_planes, h_grp, h_codes, h_scales = {}, {}, {}, {}
+        logits = {}
+
+        def load_w1(r):
+            net, g = divmod(r, ROUNDS)
+            raw = w1_raw_pool.tile([P, IN_PASSES, PACK, K_PASS], BF16, name="w1_raw")
+            for c in range(IN_PASSES):
+                nc.sync.dma_start(
+                    out=raw[:, c],
+                    in_=W1[net][c * K_PASS : (c + 1) * K_PASS, g * K_PASS : (g + 1) * K_PASS].rearrange(
+                        "(p j) w -> p j w", j=PACK
+                    ),
+                )
+            w1_raw[r] = raw
+
+        def regroup_w1(r):
+            grp = w1_grp_pool.tile([P, IN_PASSES, K_PASS, PACK], BF16, name="w1_grp", align_bytes=64)
+            regroup(nc.vector.tensor_copy, grp[:, 0], w1_raw[r][:, 0])
+            regroup(nc.scalar.copy, grp[:, 1], w1_raw[r][:, 1])
+            w1_grp[r] = grp
+
+        def quantise_w1(r):
+            codes = w1_mx_pool.tile([P, IN_PASSES, K_PASS], U32, name="w1_codes", align_bytes=64)
+            scales = w1_mx_pool.tile([P, IN_PASSES, K_PASS], U8, name="w1_scales", align_bytes=64)
+            nc.vector.quantize_mx(
+                out=codes[:].rearrange("p c w -> p (c w)").bitcast(FP8X4),
+                scales=scales[:].rearrange("p c w -> p (c w)"),
+                in_=w1_grp[r][:].rearrange("p c w j -> p (c w j)"),
+            )
+            w1_codes[r], w1_scales[r] = codes, scales
+
+        def load_w2(net):
+            raw = w2_stage.tile([P, PACK, ROUNDS * C], BF16, name="w2_raw")
+            rows = W2[net].rearrange("(g t p) n -> t p g n", t=PACK, p=P)
+            for t in range(PACK):
+                nc.sync.dma_start(out=raw[:, t, :].rearrange("p (g n) -> p g n", n=C), in_=rows[t])
+            w2_raw[net] = raw
+
+        def quantise_w2(net):
+            grp = w2_stage.tile([P, ROUNDS * C, PACK], BF16, name="w2_grp", align_bytes=64)
+            regroup(nc.vector.tensor_copy, grp[:], w2_raw[net][:])
+            codes = w2_mx_pool.tile([P, ROUNDS, C], U32, name="w2_codes", align_bytes=64)
+            scales = w2_mx_pool.tile([P, ROUNDS, C], U8, name="w2_scales", align_bytes=64)
+            nc.vector.quantize_mx(
+                out=codes[:].rearrange("p g n -> p (g n)").bitcast(FP8X4),
+                scales=scales[:].rearrange("p g n -> p (g n)"),
+                in_=grp[:].rearrange("p w t -> p (w t)"),
+            )
+            w2_codes[net], w2_scales[net] = codes, scales
+
+        def layer1(r):
+            net, g = divmod(r, ROUNDS)
+            planes = h_pool.tile([P, PACK, B], BF16, name="h_planes")
+            for t in range(PACK):
+                units = slice(t * P, (t + 1) * P)
+                acc = psum_h.tile([P, B], F32, tag="bank")
+                for c in range(IN_PASSES):
+                    nc.tensor.matmul_mx(
+                        out=acc[:],
+                        lhsT=w1_codes[r][:, c, units].bitcast(FP8X4),
+                        lhsT_scale=w1_scales[r][:, c, units],
+                        rhs=x_codes[:, c, :].bitcast(FP8X4),
+                        rhs_scale=x_scales[:, c, :],
+                        start=(c == 0),
+                        stop=(c == IN_PASSES - 1),
+                    )
+                col = net * B1_ROWS + g * PACK + t
+                nc.scalar.activation(
+                    out=planes[:, t, :], in_=acc[:], func=ACT.Relu, bias=bias_cols[:, col : col + 1], scale=1.0
+                )
+            h_planes[r] = planes
+
+        def regroup_h(r):
+            grp = h_pool.tile([P, B, PACK], BF16, name="h_grp", align_bytes=64)
+            regroup(nc.vector.tensor_copy, grp[:], h_planes[r][:])
+            h_grp[r] = grp
+
+        def quantise_h(r):
+            codes = h_pool.tile([P, B], U32, name="h_codes", align_bytes=64)
+            scales = h_pool.tile([P, B], U8, name="h_scales", align_bytes=64)
+            nc.vector.quantize_mx(
+                out=codes[:].bitcast(FP8X4), scales=scales[:], in_=h_grp[r][:].rearrange("p b t -> p (b t)")
+            )
+            h_codes[r], h_scales[r] = codes, scales
+
+        def layer2(r):
+            net, g = divmod(r, ROUNDS)
+            for i in range(B_TILES):
+                if g == 0:
+                    bank = psum_l.tile([P, C], F32, name="logits%d" % i)
+                    logits[i] = bank
+                rows = slice(i * P, (i + 1) * P)
+                nc.tensor.matmul_mx(
+                    out=logits[i][:],
+                    lhsT=h_codes[r][:, rows].bitcast(FP8X4),
+                    lhsT_scale=h_scales[r][:, rows],
+                    rhs=w2_codes[net][:, g, :].bitcast(FP8X4),
+                    rhs_scale=w2_scales[net][:, g, :],
+                    start=(g == 0),
+                    stop=(g == ROUNDS - 1),
+                )
+
+        def softmax_parts(net):
+            z = soft.tile([P, B_TILES, C], F32, name="z%d" % net)
+            for i in range(B_TILES):
+                nc.vector.tensor_tensor(out=z[:, i, :], in0=logits[i][:], in1=b2_bc[:, net, :], op=ALU.add)
+            negmax = small.tile([P, B_TILES], F32, name="negmax%d" % net)
+            nc.vector.tensor_reduce(out=negmax[:], in_=z[:], axis=AX.X, op=ALU.max, negate=True)
+            e = soft.tile([P, B_TILES, C], F32, name="e%d" % net)
+            esum = small.tile([P, B_TILES], F32, name="esum%d" % net)
+            for i in range(B_TILES):
+                nc.scalar.activation(
+                    out=e[:, i, :],
+                    in_=z[:, i, :],
+                    func=ACT.Exp,
+                    bias=negmax[:, i : i + 1],
+                    scale=1.0,
+                    accum_out=esum[:, i : i + 1],
+                )
+            rsum = small.tile([P, B_TILES], F32, name="rsum%d" % net)
+            nc.vector.reciprocal(out=rsum[:], in_=esum[:])
+            return e, rsum
+
+        def inv_poly(v, m, k):
+            b = small.tile([P, B_TILES], F32, name="inv_b%d" % k)
+            a = small.tile([P, B_TILES], F32, name="inv_a%d" % k)
+            nc.vector.tensor_scalar(out=b[:], in0=v[:], scalar1=-2.0 / m, scalar2=1.0, op0=ALU.mult, op1=ALU.add)
+            nc.vector.tensor_scalar_add(out=a[:], in0=b[:], scalar1=1.0)
+            for step in range(T2):
+                nc.vector.tensor_mul(out=b[:], in0=b[:], in1=b[:])
+                nc.vector.scalar_tensor_tensor(out=a[:], in0=b[:], scalar=1.0, in1=a[:], op0=ALU.add, op1=ALU.mult)
+            return a
+
+        def gate(e, rsum):
+            power = e
+            power_sums = []
+            for k in range(T1):
+                squared = soft.tile([P, B_TILES, C], F32, name="power%d" % k)
+                total = small.tile([P, B_TILES], F32, name="power_sum%d" % k)
+                for i in range(B_TILES):
+                    nc.scalar.activation(
+                        out=squared[:, i, :],
+                        in_=power[:, i, :],
+                        func=ACT.Square,
+                        scale=(rsum[:, i : i + 1] if k == 0 else 1.0),
+                        accum_out=total[:, i : i + 1],
+                    )
+                power = squared
+                power_sums.append(total)
+            factor = None
+            tau_power = TAU
+            for k in range(T1):
+                tau_power = tau_power * tau_power
+                m = 2.0 + TAU * TAU if k == 0 else 2.0
+                sm = small.tile([P, B_TILES], F32, name="sm%d" % k)
+                new_factor = small.tile([P, B_TILES], F32, name="factor%d" % k)
+                if factor is None:
+                    nc.vector.tensor_scalar_add(out=sm[:], in0=power_sums[k][:], scalar1=tau_power)
+                    a = inv_poly(sm, m, k)
+                    nc.vector.tensor_scalar_mul(out=new_factor[:], in0=a[:], scalar1=2.0 / m)
+                else:
+                    squared_factor = small.tile([P, B_TILES], F32, name="factor_sq%d" % k)
+                    nc.vector.tensor_mul(out=squared_factor[:], in0=factor[:], in1=factor[:])
+                    nc.vector.scalar_tensor_tensor(
+                        out=sm[:], in0=power_sums[k][:], scalar=tau_power, in1=squared_factor[:], op0=ALU.add, op1=ALU.mult
+                    )
+                    a = inv_poly(sm, m, k)
+                    nc.vector.scalar_tensor_tensor(
+                        out=new_factor[:], in0=a[:], scalar=2.0 / m, in1=squared_factor[:], op0=ALU.mult, op1=ALU.mult
+                    )
+                factor = new_factor
+            cond = small.tile([P, B_TILES], F32, name="cond")
+            nc.vector.tensor_scalar_mul(out=cond[:], in0=factor[:], scalar1=tau_power)
+            return cond
+
+        load_w1(0)
+        x_sb = const.tile([P, B_TILES, D_IN], BF16)
+        nc.sync.dma_start(out=x_sb[:], in_=x.rearrange("(i p) k -> p i k", p=P))
+        load_w1(1)
+        load_w2(0)
+        for r in range(2, RAW_BUFS):
+            load_w1(r)
+
+        warm = const.tile([P, 1], F32)
+        nc.vector.memset(warm[:], 0.0)
+        nc.scalar.activation(out=warm[:], in_=warm[:], func=ACT.Exp)
+
+        ident = const.tile([P, P], F32)
+        make_identity(nc, ident[:])
+
+        bias_rows = const.tile([P, P], BF16)
+        nc.vector.memset(bias_rows[:], 0.0)
+        for net in range(NETS):
+            nc.scalar.dma_start(
+                out=bias_rows[net * B1_ROWS : (net + 1) * B1_ROWS, :], in_=b1[net].rearrange("(r p) -> r p", p=P)
+            )
+            nc.scalar.dma_start(
+                out=bias_rows[B2_ROW + net : B2_ROW + net + 1, :], in_=b2[net].rearrange("(o c) -> o c", o=1)
+            )
+
+        regroup_w1(0)
+        load_w1(RAW_BUFS)
+
+        bias_rows_f32 = const.tile([P, P], F32)
+        nc.vector.tensor_copy(out=bias_rows_f32[:], in_=bias_rows[:])
+        bias_ps = psum_h.tile([P, P], F32, tag="bank")
+        nc.tensor.transpose(out=bias_ps[:], in_=bias_rows_f32[:], identity=ident[:])
+        bias_cols = const.tile([P, P], F32)
+        nc.vector.tensor_copy(out=bias_cols[:], in_=bias_ps[:])
+        b2_ps = psum_h.tile([P, NETS, C], F32, tag="bank")
+        for net in range(NETS):
+            nc.tensor.matmul(
+                out=b2_ps[:, net, :],
+                lhsT=bias_cols[:, B2_ROW + net : B2_ROW + net + 1].to_broadcast([P, P]),
+                rhs=ident[:],
+                start=True,
+                stop=True,
+            )
+        b2_bc = const.tile([P, NETS, C], F32)
+        nc.vector.tensor_copy(out=b2_bc[:], in_=b2_ps[:])
+
+        x_words = x_sb[:].bitcast(F32).rearrange("p i (c q u) -> p i c u q", c=IN_PASSES, u=2)
+        x_grp = const.tile([P, IN_PASSES, B, PACK], BF16, align_bytes=64)
+        x_grp_words = x_grp[:].bitcast(F32)
+        for c in range(IN_PASSES):
+            for half in range(2):
+                xt = psum_h.tile([P, 2, 2 * P], F32, tag="bank")
+                for u in range(2):
+                    for ii in range(2):
+                        nc.tensor.transpose(
+                            out=xt[:, u, ii * P : (ii + 1) * P], in_=x_words[:, 2 * half + ii, c, u, :], identity=ident[:]
+                        )
+                copy = nc.vector.tensor_copy if half == 0 else nc.scalar.copy
+                copy(
+                    out=x_grp_words[:, c, half * 2 * P : (half + 1) * 2 * P, :],
+                    in_=xt[:].rearrange("p u b -> p b u"),
+                )
+        x_codes = const.tile([P, IN_PASSES, B], U32, align_bytes=64)
+        x_scales = const.tile([P, IN_PASSES, B], U8, align_bytes=64)
+        nc.vector.quantize_mx(
+            out=x_codes[:].rearrange("p c b -> p (c b)").bitcast(FP8X4),
+            scales=x_scales[:].rearrange("p c b -> p (c b)"),
+            in_=x_grp[:].rearrange("p c b t -> p (c b t)"),
+        )
+
+        quantise_w1(0)
+        regroup_w1(1)
+        load_w1(RAW_BUFS + 1)
+
+        for s in range(TOTAL + 2):
+            if s + 2 < TOTAL:
+                regroup_w1(s + 2)
+            if s + 2 + RAW_BUFS < TOTAL:
+                load_w1(s + 2 + RAW_BUFS)
+            if s == 0:
+                quantise_w2(0)
+                load_w2(1)
+            if s == ROUNDS:
+                quantise_w2(1)
+            if s >= 2:
+                layer2(s - 2)
+            if s < TOTAL:
+                layer1(s)
+            if 1 <= s <= TOTAL:
+                regroup_h(s - 1)
+            if s + 1 < TOTAL:
+                quantise_w1(s + 1)
+            if 1 <= s <= TOTAL:
+                quantise_h(s - 1)
+            if s - 2 == ROUNDS - 1:
+                e1, rsum1 = softmax_parts(0)
+                cond = gate(e1, rsum1)
+                keep = small.tile([P, B_TILES], F32)
+                nc.vector.tensor_scalar(out=keep[:], in0=cond[:], scalar1=-1.0, scalar2=1.0, op0=ALU.mult, op1=ALU.add)
+                nc.vector.tensor_mul(out=keep[:], in0=keep[:], in1=rsum1[:])
+                share1 = soft.tile([P, B_TILES, C], F32)
+                nc.vector.tensor_tensor(
+                    out=share1[:], in0=e1[:], in1=keep[:].unsqueeze(2).to_broadcast([P, B_TILES, C]), op=ALU.mult
+                )
+
+        e2, rsum2 = softmax_parts(1)
+        weight2 = small.tile([P, B_TILES], F32)
+        nc.vector.tensor_mul(out=weight2[:], in0=cond[:], in1=rsum2[:])
+        result = soft.tile([P, B_TILES, C], F32)
+        out_tiles = out.rearrange("(i p) c -> i p c", p=P)
+        for i in range(B_TILES):
+            nc.vector.scalar_tensor_tensor(
+                out=result[:, i, :],
+                in0=e2[:, i, :],
+                scalar=weight2[:, i : i + 1],
+                in1=share1[:, i, :],
+                op0=ALU.mult,
+                op1=ALU.add,
+            )
+            nc.sync.dma_start(out=out_tiles[i], in_=result[:, i, :])

@@ -26,6 +26,7 @@ B_TILES = B // P
 B1_ROWS = D_H // P
 B2_ROW = NETS * B1_ROWS
 RAW_BUFS = 6
+W2_AHEAD = 2
 
 FLOPS = NETS * (2 * B * D_IN * D_H + 2 * B * D_H * C)
 
@@ -45,8 +46,7 @@ def tile_combnethe_pa_kernel(tc, x, W1o, b1o, W2o, b2o, W1f, b1f, W2f, b2f, out)
         w1_raw_pool = ctx.enter_context(tc.tile_pool(name="w1_raw", bufs=RAW_BUFS))
         w1_grp_pool = ctx.enter_context(tc.tile_pool(name="w1_grp", bufs=3))
         w1_mx_pool = ctx.enter_context(tc.tile_pool(name="w1_mx", bufs=3))
-        w2_stage = ctx.enter_context(tc.tile_pool(name="w2_stage", bufs=1))
-        w2_mx_pool = ctx.enter_context(tc.tile_pool(name="w2_mx", bufs=NETS))
+        w2_pool = ctx.enter_context(tc.tile_pool(name="w2", bufs=3))
         h_pool = ctx.enter_context(tc.tile_pool(name="h", bufs=3))
         soft = ctx.enter_context(tc.tile_pool(name="soft", bufs=1))
         small = ctx.enter_context(tc.tile_pool(name="small", bufs=1))
@@ -54,9 +54,10 @@ def tile_combnethe_pa_kernel(tc, x, W1o, b1o, W2o, b2o, W1f, b1f, W2f, b2f, out)
         psum_l = ctx.enter_context(tc.psum_pool(name="psum_l", bufs=1))
 
         w1_raw, w1_grp, w1_codes, w1_scales = {}, {}, {}, {}
-        w2_raw, w2_codes, w2_scales = {}, {}, {}
-        h_planes, h_grp, h_codes, h_scales = {}, {}, {}, {}
+        w2_raw, w2_grp, w2_codes, w2_scales = {}, {}, {}, {}
+        h_banks, h_planes, h_grp, h_codes, h_scales = {}, {}, {}, {}, {}
         logits = {}
+        power_sums, factors = [], []
 
         def load_w1(r):
             net, g = divmod(r, ROUNDS)
@@ -86,28 +87,29 @@ def tile_combnethe_pa_kernel(tc, x, W1o, b1o, W2o, b2o, W1f, b1f, W2f, b2f, out)
             )
             w1_codes[r], w1_scales[r] = codes, scales
 
-        def load_w2(net):
-            raw = w2_stage.tile([P, PACK, ROUNDS * C], BF16, name="w2_raw")
-            rows = W2[net].rearrange("(g t p) n -> t p g n", t=PACK, p=P)
-            for t in range(PACK):
-                nc.sync.dma_start(out=raw[:, t, :].rearrange("p (g n) -> p g n", n=C), in_=rows[t])
-            w2_raw[net] = raw
-
-        def quantise_w2(net):
-            grp = w2_stage.tile([P, ROUNDS * C, PACK], BF16, name="w2_grp", align_bytes=64)
-            regroup(nc.vector.tensor_copy, grp[:], w2_raw[net][:])
-            codes = w2_mx_pool.tile([P, ROUNDS, C], U32, name="w2_codes", align_bytes=64)
-            scales = w2_mx_pool.tile([P, ROUNDS, C], U8, name="w2_scales", align_bytes=64)
-            nc.vector.quantize_mx(
-                out=codes[:].rearrange("p g n -> p (g n)").bitcast(FP8X4),
-                scales=scales[:].rearrange("p g n -> p (g n)"),
-                in_=grp[:].rearrange("p w t -> p (w t)"),
-            )
-            w2_codes[net], w2_scales[net] = codes, scales
-
-        def layer1(r):
+        def load_w2(r):
             net, g = divmod(r, ROUNDS)
-            planes = h_pool.tile([P, PACK, B], BF16, name="h_planes")
+            raw = w2_pool.tile([P, PACK, C], BF16, name="w2_raw")
+            nc.sync.dma_start(
+                out=raw[:], in_=W2[net][g * K_PASS : (g + 1) * K_PASS, :].rearrange("(t p) n -> p t n", p=P)
+            )
+            w2_raw[r] = raw
+
+        def regroup_w2(r):
+            grp = w2_pool.tile([P, C, PACK], BF16, name="w2_grp", align_bytes=64)
+            regroup(nc.vector.tensor_copy, grp[:], w2_raw[r][:])
+            w2_grp[r] = grp
+
+        def quantise_w2(r):
+            codes = w2_pool.tile([P, C], U32, name="w2_codes", align_bytes=64)
+            scales = w2_pool.tile([P, C], U8, name="w2_scales", align_bytes=64)
+            nc.vector.quantize_mx(
+                out=codes[:].bitcast(FP8X4), scales=scales[:], in_=w2_grp[r][:].rearrange("p n t -> p (n t)")
+            )
+            w2_codes[r], w2_scales[r] = codes, scales
+
+        def layer1_passes(r):
+            h_banks[r] = []
             for t in range(PACK):
                 units = slice(t * P, (t + 1) * P)
                 acc = psum_h.tile([P, B], F32, tag="bank")
@@ -121,9 +123,18 @@ def tile_combnethe_pa_kernel(tc, x, W1o, b1o, W2o, b2o, W1f, b1f, W2f, b2f, out)
                         start=(c == 0),
                         stop=(c == IN_PASSES - 1),
                     )
-                col = net * B1_ROWS + g * PACK + t
+                h_banks[r].append(acc)
+
+        def layer1_exits(r):
+            planes = h_pool.tile([P, PACK, B], BF16, name="h_planes")
+            for t in range(PACK):
+                col = r * PACK + t
                 nc.scalar.activation(
-                    out=planes[:, t, :], in_=acc[:], func=ACT.Relu, bias=bias_cols[:, col : col + 1], scale=1.0
+                    out=planes[:, t, :],
+                    in_=h_banks[r][t][:],
+                    func=ACT.Relu,
+                    bias=bias_cols[:, col : col + 1],
+                    scale=1.0,
                 )
             h_planes[r] = planes
 
@@ -151,21 +162,22 @@ def tile_combnethe_pa_kernel(tc, x, W1o, b1o, W2o, b2o, W1f, b1f, W2f, b2f, out)
                     out=logits[i][:],
                     lhsT=h_codes[r][:, rows].bitcast(FP8X4),
                     lhsT_scale=h_scales[r][:, rows],
-                    rhs=w2_codes[net][:, g, :].bitcast(FP8X4),
-                    rhs_scale=w2_scales[net][:, g, :],
+                    rhs=w2_codes[r][:].bitcast(FP8X4),
+                    rhs_scale=w2_scales[r][:],
                     start=(g == 0),
                     stop=(g == ROUNDS - 1),
                 )
 
         def softmax_parts(net):
             z = soft.tile([P, B_TILES, C], F32, name="z%d" % net)
-            for i in range(B_TILES):
-                nc.vector.tensor_tensor(out=z[:, i, :], in0=logits[i][:], in1=b2_bc[:, net, :], op=ALU.add)
             negmax = small.tile([P, B_TILES], F32, name="negmax%d" % net)
-            nc.vector.tensor_reduce(out=negmax[:], in_=z[:], axis=AX.X, op=ALU.max, negate=True)
             e = soft.tile([P, B_TILES, C], F32, name="e%d" % net)
             esum = small.tile([P, B_TILES], F32, name="esum%d" % net)
             for i in range(B_TILES):
+                nc.vector.tensor_tensor(out=z[:, i, :], in0=logits[i][:], in1=b2_bc[:, net, :], op=ALU.add)
+                nc.vector.tensor_reduce(
+                    out=negmax[:, i : i + 1], in_=z[:, i, :], axis=AX.X, op=ALU.max, negate=True
+                )
                 nc.scalar.activation(
                     out=e[:, i, :],
                     in_=z[:, i, :],
@@ -174,9 +186,7 @@ def tile_combnethe_pa_kernel(tc, x, W1o, b1o, W2o, b2o, W1f, b1f, W2f, b2f, out)
                     scale=1.0,
                     accum_out=esum[:, i : i + 1],
                 )
-            rsum = small.tile([P, B_TILES], F32, name="rsum%d" % net)
-            nc.vector.reciprocal(out=rsum[:], in_=esum[:])
-            return e, rsum
+            return e, esum
 
         def inv_poly(v, m, k):
             b = small.tile([P, B_TILES], F32, name="inv_b%d" % k)
@@ -188,9 +198,8 @@ def tile_combnethe_pa_kernel(tc, x, W1o, b1o, W2o, b2o, W1f, b1f, W2f, b2f, out)
                 nc.vector.scalar_tensor_tensor(out=a[:], in0=b[:], scalar=1.0, in1=a[:], op0=ALU.add, op1=ALU.mult)
             return a
 
-        def gate(e, rsum):
+        def sum_powers(e, rsum):
             power = e
-            power_sums = []
             for k in range(T1):
                 squared = soft.tile([P, B_TILES, C], F32, name="power%d" % k)
                 total = small.tile([P, B_TILES], F32, name="power_sum%d" % k)
@@ -204,39 +213,43 @@ def tile_combnethe_pa_kernel(tc, x, W1o, b1o, W2o, b2o, W1f, b1f, W2f, b2f, out)
                     )
                 power = squared
                 power_sums.append(total)
-            factor = None
-            tau_power = TAU
-            for k in range(T1):
-                tau_power = tau_power * tau_power
-                m = 2.0 + TAU * TAU if k == 0 else 2.0
-                sm = small.tile([P, B_TILES], F32, name="sm%d" % k)
-                new_factor = small.tile([P, B_TILES], F32, name="factor%d" % k)
-                if factor is None:
-                    nc.vector.tensor_scalar_add(out=sm[:], in0=power_sums[k][:], scalar1=tau_power)
-                    a = inv_poly(sm, m, k)
-                    nc.vector.tensor_scalar_mul(out=new_factor[:], in0=a[:], scalar1=2.0 / m)
-                else:
-                    squared_factor = small.tile([P, B_TILES], F32, name="factor_sq%d" % k)
-                    nc.vector.tensor_mul(out=squared_factor[:], in0=factor[:], in1=factor[:])
-                    nc.vector.scalar_tensor_tensor(
-                        out=sm[:], in0=power_sums[k][:], scalar=tau_power, in1=squared_factor[:], op0=ALU.add, op1=ALU.mult
-                    )
-                    a = inv_poly(sm, m, k)
-                    nc.vector.scalar_tensor_tensor(
-                        out=new_factor[:], in0=a[:], scalar=2.0 / m, in1=squared_factor[:], op0=ALU.mult, op1=ALU.mult
-                    )
-                factor = new_factor
-            cond = small.tile([P, B_TILES], F32, name="cond")
-            nc.vector.tensor_scalar_mul(out=cond[:], in0=factor[:], scalar1=tau_power)
-            return cond
 
-        load_w1(0)
+        def gate_round(k):
+            tau_power = TAU ** (2 ** (k + 1))
+            m = 2.0 + TAU * TAU if k == 0 else 2.0
+            sm = small.tile([P, B_TILES], F32, name="sm%d" % k)
+            factor = small.tile([P, B_TILES], F32, name="factor%d" % k)
+            if k == 0:
+                nc.vector.tensor_scalar_add(out=sm[:], in0=power_sums[k][:], scalar1=tau_power)
+                a = inv_poly(sm, m, k)
+                nc.vector.tensor_scalar_mul(out=factor[:], in0=a[:], scalar1=2.0 / m)
+            else:
+                squared_factor = small.tile([P, B_TILES], F32, name="factor_sq%d" % k)
+                nc.vector.tensor_mul(out=squared_factor[:], in0=factors[k - 1][:], in1=factors[k - 1][:])
+                nc.vector.scalar_tensor_tensor(
+                    out=sm[:], in0=power_sums[k][:], scalar=tau_power, in1=squared_factor[:], op0=ALU.add, op1=ALU.mult
+                )
+                a = inv_poly(sm, m, k)
+                nc.vector.scalar_tensor_tensor(
+                    out=factor[:], in0=a[:], scalar=2.0 / m, in1=squared_factor[:], op0=ALU.mult, op1=ALU.mult
+                )
+            factors.append(factor)
+
         x_sb = const.tile([P, B_TILES, D_IN], BF16)
         nc.sync.dma_start(out=x_sb[:], in_=x.rearrange("(i p) k -> p i k", p=P))
-        load_w1(1)
-        load_w2(0)
-        for r in range(2, RAW_BUFS):
+        bias_rows = const.tile([P, P], BF16)
+        nc.vector.memset(bias_rows[:], 0.0)
+        for net in range(NETS):
+            nc.sync.dma_start(
+                out=bias_rows[net * B1_ROWS : (net + 1) * B1_ROWS, :], in_=b1[net].rearrange("(r p) -> r p", p=P)
+            )
+            nc.sync.dma_start(
+                out=bias_rows[B2_ROW + net : B2_ROW + net + 1, :], in_=b2[net].rearrange("(o c) -> o c", o=1)
+            )
+        for r in range(RAW_BUFS):
             load_w1(r)
+            if r < W2_AHEAD:
+                load_w2(r)
 
         warm = const.tile([P, 1], F32)
         nc.vector.memset(warm[:], 0.0)
@@ -245,36 +258,8 @@ def tile_combnethe_pa_kernel(tc, x, W1o, b1o, W2o, b2o, W1f, b1f, W2f, b2f, out)
         ident = const.tile([P, P], F32)
         make_identity(nc, ident[:])
 
-        bias_rows = const.tile([P, P], BF16)
-        nc.vector.memset(bias_rows[:], 0.0)
-        for net in range(NETS):
-            nc.scalar.dma_start(
-                out=bias_rows[net * B1_ROWS : (net + 1) * B1_ROWS, :], in_=b1[net].rearrange("(r p) -> r p", p=P)
-            )
-            nc.scalar.dma_start(
-                out=bias_rows[B2_ROW + net : B2_ROW + net + 1, :], in_=b2[net].rearrange("(o c) -> o c", o=1)
-            )
-
-        regroup_w1(0)
-        load_w1(RAW_BUFS)
-
         bias_rows_f32 = const.tile([P, P], F32)
         nc.vector.tensor_copy(out=bias_rows_f32[:], in_=bias_rows[:])
-        bias_ps = psum_h.tile([P, P], F32, tag="bank")
-        nc.tensor.transpose(out=bias_ps[:], in_=bias_rows_f32[:], identity=ident[:])
-        bias_cols = const.tile([P, P], F32)
-        nc.vector.tensor_copy(out=bias_cols[:], in_=bias_ps[:])
-        b2_ps = psum_h.tile([P, NETS, C], F32, tag="bank")
-        for net in range(NETS):
-            nc.tensor.matmul(
-                out=b2_ps[:, net, :],
-                lhsT=bias_cols[:, B2_ROW + net : B2_ROW + net + 1].to_broadcast([P, P]),
-                rhs=ident[:],
-                start=True,
-                stop=True,
-            )
-        b2_bc = const.tile([P, NETS, C], F32)
-        nc.vector.tensor_copy(out=b2_bc[:], in_=b2_ps[:])
 
         x_words = x_sb[:].bitcast(F32).rearrange("p i (c q u) -> p i c u q", c=IN_PASSES, u=2)
         x_grp = const.tile([P, IN_PASSES, B, PACK], BF16, align_bytes=64)
@@ -292,6 +277,12 @@ def tile_combnethe_pa_kernel(tc, x, W1o, b1o, W2o, b2o, W1f, b1f, W2f, b2f, out)
                     out=x_grp_words[:, c, half * 2 * P : (half + 1) * 2 * P, :],
                     in_=xt[:].rearrange("p u b -> p b u"),
                 )
+
+        bias_ps = psum_h.tile([P, P], F32, tag="bank")
+        nc.tensor.transpose(out=bias_ps[:], in_=bias_rows_f32[:], identity=ident[:])
+        bias_cols = const.tile([P, P], F32)
+        nc.vector.tensor_copy(out=bias_cols[:], in_=bias_ps[:])
+
         x_codes = const.tile([P, IN_PASSES, B], U32, align_bytes=64)
         x_scales = const.tile([P, IN_PASSES, B], U8, align_bytes=64)
         nc.vector.quantize_mx(
@@ -300,33 +291,58 @@ def tile_combnethe_pa_kernel(tc, x, W1o, b1o, W2o, b2o, W1f, b1f, W2f, b2f, out)
             in_=x_grp[:].rearrange("p c b t -> p (c b t)"),
         )
 
-        quantise_w1(0)
-        regroup_w1(1)
-        load_w1(RAW_BUFS + 1)
+        b2_ps = psum_h.tile([P, NETS, C], F32, tag="bank")
+        for net in range(NETS):
+            nc.tensor.matmul(
+                out=b2_ps[:, net, :],
+                lhsT=bias_cols[:, B2_ROW + net : B2_ROW + net + 1].to_broadcast([P, P]),
+                rhs=ident[:],
+                start=True,
+                stop=True,
+            )
+        b2_bc = const.tile([P, NETS, C], F32)
+        nc.vector.tensor_copy(out=b2_bc[:], in_=b2_ps[:])
 
-        for s in range(TOTAL + 2):
-            if s + 2 < TOTAL:
-                regroup_w1(s + 2)
-            if s + 2 + RAW_BUFS < TOTAL:
-                load_w1(s + 2 + RAW_BUFS)
-            if s == 0:
-                quantise_w2(0)
-                load_w2(1)
-            if s == ROUNDS:
-                quantise_w2(1)
-            if s >= 2:
-                layer2(s - 2)
-            if s < TOTAL:
-                layer1(s)
-            if 1 <= s <= TOTAL:
-                regroup_h(s - 1)
+        for r in range(2):
+            regroup_w1(r)
+            load_w1(r + RAW_BUFS)
+        quantise_w1(0)
+        layer1_passes(0)
+
+        GATE_START = ROUNDS
+        for s in range(TOTAL + 1):
             if s + 1 < TOTAL:
                 quantise_w1(s + 1)
-            if 1 <= s <= TOTAL:
+            if s >= 1:
                 quantise_h(s - 1)
-            if s - 2 == ROUNDS - 1:
-                e1, rsum1 = softmax_parts(0)
-                cond = gate(e1, rsum1)
+            if s < TOTAL:
+                regroup_w2(s)
+                layer1_exits(s)
+            if s + 2 < TOTAL:
+                regroup_w1(s + 2)
+            if s + W2_AHEAD < TOTAL:
+                load_w2(s + W2_AHEAD)
+            if s + 2 + RAW_BUFS < TOTAL:
+                load_w1(s + 2 + RAW_BUFS)
+            if s + 1 < TOTAL:
+                layer1_passes(s + 1)
+            if s < TOTAL:
+                quantise_w2(s)
+            if s >= 1:
+                layer2(s - 1)
+            if s < TOTAL:
+                regroup_h(s)
+            if s == GATE_START:
+                e1, esum1 = softmax_parts(0)
+            if s == GATE_START + 1:
+                rsum1 = small.tile([P, B_TILES], F32)
+                nc.vector.reciprocal(out=rsum1[:], in_=esum1[:])
+                sum_powers(e1, rsum1)
+            if GATE_START + 2 <= s < GATE_START + 2 + T1:
+                gate_round(s - GATE_START - 2)
+            if s == GATE_START + 2 + T1:
+                cond = small.tile([P, B_TILES], F32)
+                nc.vector.tensor_scalar_mul(out=cond[:], in0=factors[T1 - 1][:], scalar1=TAU ** (2**T1))
                 keep = small.tile([P, B_TILES], F32)
                 nc.vector.tensor_scalar(out=keep[:], in0=cond[:], scalar1=-1.0, scalar2=1.0, op0=ALU.mult, op1=ALU.add)
                 nc.vector.tensor_mul(out=keep[:], in0=keep[:], in1=rsum1[:])
@@ -335,12 +351,13 @@ def tile_combnethe_pa_kernel(tc, x, W1o, b1o, W2o, b2o, W1f, b1f, W2f, b2f, out)
                     out=share1[:], in0=e1[:], in1=keep[:].unsqueeze(2).to_broadcast([P, B_TILES, C]), op=ALU.mult
                 )
 
-        e2, rsum2 = softmax_parts(1)
+        e2, esum2 = softmax_parts(1)
         weight2 = small.tile([P, B_TILES], F32)
-        nc.vector.tensor_mul(out=weight2[:], in0=cond[:], in1=rsum2[:])
         result = soft.tile([P, B_TILES, C], F32)
         out_tiles = out.rearrange("(i p) c -> i p c", p=P)
         for i in range(B_TILES):
+            nc.vector.reciprocal(out=weight2[:, i : i + 1], in_=esum2[:, i : i + 1])
+            nc.vector.tensor_mul(out=weight2[:, i : i + 1], in0=weight2[:, i : i + 1], in1=cond[:, i : i + 1])
             nc.vector.scalar_tensor_tensor(
                 out=result[:, i, :],
                 in0=e2[:, i, :],

@@ -18,6 +18,7 @@ K_PASS = P * PACK
 
 B, D_IN, D_H, C = 512, 1024, 4096, 128
 TAU, T1, T2 = 0.5, 3, 3
+TAU_LAST = TAU ** (2**T1)
 NETS = 2
 IN_PASSES = D_IN // K_PASS
 ROUNDS = D_H // K_PASS
@@ -57,7 +58,7 @@ def tile_combnethe_pa_kernel(tc, x, W1o, b1o, W2o, b2o, W1f, b1f, W2f, b2f, out)
         w2_raw, w2_grp, w2_codes, w2_scales = {}, {}, {}, {}
         h_banks, h_planes, h_grp, h_codes, h_scales = {}, {}, {}, {}, {}
         logits = {}
-        power_sums, factors = [], []
+        power_sums, factors, small_ops = [], [], []
 
         def load_w1(r):
             net, g = divmod(r, ROUNDS)
@@ -74,6 +75,7 @@ def tile_combnethe_pa_kernel(tc, x, W1o, b1o, W2o, b2o, W1f, b1f, W2f, b2f, out)
         def regroup_w1(r):
             grp = w1_grp_pool.tile([P, IN_PASSES, K_PASS, PACK], BF16, name="w1_grp", align_bytes=64)
             regroup(nc.vector.tensor_copy, grp[:, 0], w1_raw[r][:, 0])
+            one_small_op()
             regroup(nc.scalar.copy, grp[:, 1], w1_raw[r][:, 1])
             w1_grp[r] = grp
 
@@ -85,6 +87,7 @@ def tile_combnethe_pa_kernel(tc, x, W1o, b1o, W2o, b2o, W1f, b1f, W2f, b2f, out)
                 scales=scales[:].rearrange("p c w -> p (c w)"),
                 in_=w1_grp[r][:].rearrange("p c w j -> p (c w j)"),
             )
+            one_small_op()
             w1_codes[r], w1_scales[r] = codes, scales
 
         def load_w2(r):
@@ -98,6 +101,7 @@ def tile_combnethe_pa_kernel(tc, x, W1o, b1o, W2o, b2o, W1f, b1f, W2f, b2f, out)
         def regroup_w2(r):
             grp = w2_pool.tile([P, C, PACK], BF16, name="w2_grp", align_bytes=64)
             regroup(nc.vector.tensor_copy, grp[:], w2_raw[r][:])
+            one_small_op()
             w2_grp[r] = grp
 
         def quantise_w2(r):
@@ -106,6 +110,7 @@ def tile_combnethe_pa_kernel(tc, x, W1o, b1o, W2o, b2o, W1f, b1f, W2f, b2f, out)
             nc.vector.quantize_mx(
                 out=codes[:].bitcast(FP8X4), scales=scales[:], in_=w2_grp[r][:].rearrange("p n t -> p (n t)")
             )
+            one_small_op()
             w2_codes[r], w2_scales[r] = codes, scales
 
         def layer1_passes(r):
@@ -141,6 +146,7 @@ def tile_combnethe_pa_kernel(tc, x, W1o, b1o, W2o, b2o, W1f, b1f, W2f, b2f, out)
         def regroup_h(r):
             grp = h_pool.tile([P, B, PACK], BF16, name="h_grp", align_bytes=64)
             regroup(nc.vector.tensor_copy, grp[:], h_planes[r][:])
+            one_small_op()
             h_grp[r] = grp
 
         def quantise_h(r):
@@ -149,6 +155,7 @@ def tile_combnethe_pa_kernel(tc, x, W1o, b1o, W2o, b2o, W1f, b1f, W2f, b2f, out)
             nc.vector.quantize_mx(
                 out=codes[:].bitcast(FP8X4), scales=scales[:], in_=h_grp[r][:].rearrange("p b t -> p (b t)")
             )
+            one_small_op()
             h_codes[r], h_scales[r] = codes, scales
 
         def layer2(r):
@@ -188,14 +195,21 @@ def tile_combnethe_pa_kernel(tc, x, W1o, b1o, W2o, b2o, W1f, b1f, W2f, b2f, out)
                 )
             return e, esum
 
+        def later(op, **operands):
+            small_ops.append(lambda: op(**operands))
+
+        def one_small_op():
+            if small_ops:
+                small_ops.pop(0)()
+
         def inv_poly(v, m, k):
             b = small.tile([P, B_TILES], F32, name="inv_b%d" % k)
             a = small.tile([P, B_TILES], F32, name="inv_a%d" % k)
-            nc.vector.tensor_scalar(out=b[:], in0=v[:], scalar1=-2.0 / m, scalar2=1.0, op0=ALU.mult, op1=ALU.add)
-            nc.vector.tensor_scalar_add(out=a[:], in0=b[:], scalar1=1.0)
+            later(nc.vector.tensor_scalar, out=b[:], in0=v[:], scalar1=-2.0 / m, scalar2=1.0, op0=ALU.mult, op1=ALU.add)
+            later(nc.vector.tensor_scalar_add, out=a[:], in0=b[:], scalar1=1.0)
             for step in range(T2):
-                nc.vector.tensor_mul(out=b[:], in0=b[:], in1=b[:])
-                nc.vector.scalar_tensor_tensor(out=a[:], in0=b[:], scalar=1.0, in1=a[:], op0=ALU.add, op1=ALU.mult)
+                later(nc.vector.tensor_mul, out=b[:], in0=b[:], in1=b[:])
+                later(nc.vector.scalar_tensor_tensor, out=a[:], in0=b[:], scalar=1.0, in1=a[:], op0=ALU.add, op1=ALU.mult)
             return a
 
         def sum_powers(e, rsum):
@@ -220,18 +234,30 @@ def tile_combnethe_pa_kernel(tc, x, W1o, b1o, W2o, b2o, W1f, b1f, W2f, b2f, out)
             sm = small.tile([P, B_TILES], F32, name="sm%d" % k)
             factor = small.tile([P, B_TILES], F32, name="factor%d" % k)
             if k == 0:
-                nc.vector.tensor_scalar_add(out=sm[:], in0=power_sums[k][:], scalar1=tau_power)
+                later(nc.vector.tensor_scalar_add, out=sm[:], in0=power_sums[k][:], scalar1=tau_power)
                 a = inv_poly(sm, m, k)
-                nc.vector.tensor_scalar_mul(out=factor[:], in0=a[:], scalar1=2.0 / m)
+                later(nc.vector.tensor_scalar_mul, out=factor[:], in0=a[:], scalar1=2.0 / m)
             else:
                 squared_factor = small.tile([P, B_TILES], F32, name="factor_sq%d" % k)
-                nc.vector.tensor_mul(out=squared_factor[:], in0=factors[k - 1][:], in1=factors[k - 1][:])
-                nc.vector.scalar_tensor_tensor(
-                    out=sm[:], in0=power_sums[k][:], scalar=tau_power, in1=squared_factor[:], op0=ALU.add, op1=ALU.mult
+                later(nc.vector.tensor_mul, out=squared_factor[:], in0=factors[k - 1][:], in1=factors[k - 1][:])
+                later(
+                    nc.vector.scalar_tensor_tensor,
+                    out=sm[:],
+                    in0=power_sums[k][:],
+                    scalar=tau_power,
+                    in1=squared_factor[:],
+                    op0=ALU.add,
+                    op1=ALU.mult,
                 )
                 a = inv_poly(sm, m, k)
-                nc.vector.scalar_tensor_tensor(
-                    out=factor[:], in0=a[:], scalar=2.0 / m, in1=squared_factor[:], op0=ALU.mult, op1=ALU.mult
+                later(
+                    nc.vector.scalar_tensor_tensor,
+                    out=factor[:],
+                    in0=a[:],
+                    scalar=2.0 / m,
+                    in1=squared_factor[:],
+                    op0=ALU.mult,
+                    op1=ALU.mult,
                 )
             factors.append(factor)
 
@@ -334,18 +360,24 @@ def tile_combnethe_pa_kernel(tc, x, W1o, b1o, W2o, b2o, W1f, b1f, W2f, b2f, out)
                 regroup_h(s)
             if s == GATE_START:
                 e1, esum1 = softmax_parts(0)
-            if s == GATE_START + 1:
                 rsum1 = small.tile([P, B_TILES], F32)
                 nc.vector.reciprocal(out=rsum1[:], in_=esum1[:])
                 sum_powers(e1, rsum1)
-            if GATE_START + 2 <= s < GATE_START + 2 + T1:
-                gate_round(s - GATE_START - 2)
-            if s == GATE_START + 2 + T1:
-                cond = small.tile([P, B_TILES], F32)
-                nc.vector.tensor_scalar_mul(out=cond[:], in0=factors[T1 - 1][:], scalar1=TAU ** (2**T1))
+                for k in range(T1):
+                    gate_round(k)
                 keep = small.tile([P, B_TILES], F32)
-                nc.vector.tensor_scalar(out=keep[:], in0=cond[:], scalar1=-1.0, scalar2=1.0, op0=ALU.mult, op1=ALU.add)
-                nc.vector.tensor_mul(out=keep[:], in0=keep[:], in1=rsum1[:])
+                later(
+                    nc.vector.tensor_scalar,
+                    out=keep[:],
+                    in0=factors[T1 - 1][:],
+                    scalar1=-TAU_LAST,
+                    scalar2=1.0,
+                    op0=ALU.mult,
+                    op1=ALU.add,
+                )
+                later(nc.vector.tensor_mul, out=keep[:], in0=keep[:], in1=rsum1[:])
+            if s == TOTAL - 1:
+                assert not small_ops
                 share1 = soft.tile([P, B_TILES, C], F32)
                 nc.vector.tensor_tensor(
                     out=share1[:], in0=e1[:], in1=keep[:].unsqueeze(2).to_broadcast([P, B_TILES, C]), op=ALU.mult
@@ -357,7 +389,14 @@ def tile_combnethe_pa_kernel(tc, x, W1o, b1o, W2o, b2o, W1f, b1f, W2f, b2f, out)
         out_tiles = out.rearrange("(i p) c -> i p c", p=P)
         for i in range(B_TILES):
             nc.vector.reciprocal(out=weight2[:, i : i + 1], in_=esum2[:, i : i + 1])
-            nc.vector.tensor_mul(out=weight2[:, i : i + 1], in0=weight2[:, i : i + 1], in1=cond[:, i : i + 1])
+            nc.vector.scalar_tensor_tensor(
+                out=weight2[:, i : i + 1],
+                in0=weight2[:, i : i + 1],
+                scalar=TAU_LAST,
+                in1=factors[T1 - 1][:, i : i + 1],
+                op0=ALU.mult,
+                op1=ALU.mult,
+            )
             nc.vector.scalar_tensor_tensor(
                 out=result[:, i, :],
                 in0=e2[:, i, :],

@@ -18,7 +18,6 @@ K_PASS = P * PACK
 
 B, D_IN, D_H, C = 512, 1024, 4096, 128
 TAU, T1, T2 = 0.5, 3, 3
-TAU_LAST = TAU ** (2**T1)
 NETS = 2
 IN_PASSES = D_IN // K_PASS
 ROUNDS = D_H // K_PASS
@@ -27,6 +26,7 @@ B_TILES = B // P
 B1_ROWS = D_H // P
 B2_ROW = NETS * B1_ROWS
 RAW_BUFS = 6
+LAST_ROUND_PARTS = 2
 W2_AHEAD = 2
 
 FLOPS = NETS * (2 * B * D_IN * D_H + 2 * B * D_H * C)
@@ -58,7 +58,7 @@ def tile_combnethe_pa_kernel(tc, x, W1o, b1o, W2o, b2o, W1f, b1f, W2f, b2f, out)
         w2_raw, w2_grp, w2_codes, w2_scales = {}, {}, {}, {}
         h_banks, h_planes, h_grp, h_codes, h_scales = {}, {}, {}, {}, {}
         logits = {}
-        power_sums, factors, small_ops = [], [], []
+        power_sums, factors = [], []
 
         def load_w1(r):
             net, g = divmod(r, ROUNDS)
@@ -75,7 +75,6 @@ def tile_combnethe_pa_kernel(tc, x, W1o, b1o, W2o, b2o, W1f, b1f, W2f, b2f, out)
         def regroup_w1(r):
             grp = w1_grp_pool.tile([P, IN_PASSES, K_PASS, PACK], BF16, name="w1_grp", align_bytes=64)
             regroup(nc.vector.tensor_copy, grp[:, 0], w1_raw[r][:, 0])
-            one_small_op()
             regroup(nc.scalar.copy, grp[:, 1], w1_raw[r][:, 1])
             w1_grp[r] = grp
 
@@ -87,7 +86,6 @@ def tile_combnethe_pa_kernel(tc, x, W1o, b1o, W2o, b2o, W1f, b1f, W2f, b2f, out)
                 scales=scales[:].rearrange("p c w -> p (c w)"),
                 in_=w1_grp[r][:].rearrange("p c w j -> p (c w j)"),
             )
-            one_small_op()
             w1_codes[r], w1_scales[r] = codes, scales
 
         def load_w2(r):
@@ -101,7 +99,6 @@ def tile_combnethe_pa_kernel(tc, x, W1o, b1o, W2o, b2o, W1f, b1f, W2f, b2f, out)
         def regroup_w2(r):
             grp = w2_pool.tile([P, C, PACK], BF16, name="w2_grp", align_bytes=64)
             regroup(nc.vector.tensor_copy, grp[:], w2_raw[r][:])
-            one_small_op()
             w2_grp[r] = grp
 
         def quantise_w2(r):
@@ -110,52 +107,59 @@ def tile_combnethe_pa_kernel(tc, x, W1o, b1o, W2o, b2o, W1f, b1f, W2f, b2f, out)
             nc.vector.quantize_mx(
                 out=codes[:].bitcast(FP8X4), scales=scales[:], in_=w2_grp[r][:].rearrange("p n t -> p (n t)")
             )
-            one_small_op()
             w2_codes[r], w2_scales[r] = codes, scales
+
+        def batch_parts(r):
+            n = LAST_ROUND_PARTS if r == TOTAL - 1 else 1
+            return [slice(k * B // n, (k + 1) * B // n) for k in range(n)]
 
         def layer1_passes(r):
             h_banks[r] = []
-            for t in range(PACK):
-                units = slice(t * P, (t + 1) * P)
-                acc = psum_h.tile([P, B], F32, tag="bank")
-                for c in range(IN_PASSES):
-                    nc.tensor.matmul_mx(
-                        out=acc[:],
-                        lhsT=w1_codes[r][:, c, units].bitcast(FP8X4),
-                        lhsT_scale=w1_scales[r][:, c, units],
-                        rhs=x_codes[:, c, :].bitcast(FP8X4),
-                        rhs_scale=x_scales[:, c, :],
-                        start=(c == 0),
-                        stop=(c == IN_PASSES - 1),
-                    )
-                h_banks[r].append(acc)
+            for rows in batch_parts(r):
+                for t in range(PACK):
+                    units = slice(t * P, (t + 1) * P)
+                    acc = psum_h.tile([P, B // len(batch_parts(r))], F32, tag="bank")
+                    for c in range(IN_PASSES):
+                        nc.tensor.matmul_mx(
+                            out=acc[:],
+                            lhsT=w1_codes[r][:, c, units].bitcast(FP8X4),
+                            lhsT_scale=w1_scales[r][:, c, units],
+                            rhs=x_codes[:, c, rows].bitcast(FP8X4),
+                            rhs_scale=x_scales[:, c, rows],
+                            start=(c == 0),
+                            stop=(c == IN_PASSES - 1),
+                        )
+                    h_banks[r].append(acc)
 
         def layer1_exits(r):
             planes = h_pool.tile([P, PACK, B], BF16, name="h_planes")
-            for t in range(PACK):
-                col = r * PACK + t
-                nc.scalar.activation(
-                    out=planes[:, t, :],
-                    in_=h_banks[r][t][:],
-                    func=ACT.Relu,
-                    bias=bias_cols[:, col : col + 1],
-                    scale=1.0,
-                )
+            for k, rows in enumerate(batch_parts(r)):
+                for t in range(PACK):
+                    col = r * PACK + t
+                    nc.scalar.activation(
+                        out=planes[:, t, rows],
+                        in_=h_banks[r][k * PACK + t][:],
+                        func=ACT.Relu,
+                        bias=bias_cols[:, col : col + 1],
+                        scale=1.0,
+                    )
             h_planes[r] = planes
 
         def regroup_h(r):
             grp = h_pool.tile([P, B, PACK], BF16, name="h_grp", align_bytes=64)
-            regroup(nc.vector.tensor_copy, grp[:], h_planes[r][:])
-            one_small_op()
+            for rows in batch_parts(r):
+                regroup(nc.vector.tensor_copy, grp[:, rows, :], h_planes[r][:, :, rows])
             h_grp[r] = grp
 
         def quantise_h(r):
             codes = h_pool.tile([P, B], U32, name="h_codes", align_bytes=64)
             scales = h_pool.tile([P, B], U8, name="h_scales", align_bytes=64)
-            nc.vector.quantize_mx(
-                out=codes[:].bitcast(FP8X4), scales=scales[:], in_=h_grp[r][:].rearrange("p b t -> p (b t)")
-            )
-            one_small_op()
+            for rows in batch_parts(r):
+                nc.vector.quantize_mx(
+                    out=codes[:, rows].bitcast(FP8X4),
+                    scales=scales[:, rows],
+                    in_=h_grp[r][:, rows, :].rearrange("p b t -> p (b t)"),
+                )
             h_codes[r], h_scales[r] = codes, scales
 
         def layer2(r):
@@ -195,21 +199,14 @@ def tile_combnethe_pa_kernel(tc, x, W1o, b1o, W2o, b2o, W1f, b1f, W2f, b2f, out)
                 )
             return e, esum
 
-        def later(op, **operands):
-            small_ops.append(lambda: op(**operands))
-
-        def one_small_op():
-            if small_ops:
-                small_ops.pop(0)()
-
         def inv_poly(v, m, k):
             b = small.tile([P, B_TILES], F32, name="inv_b%d" % k)
             a = small.tile([P, B_TILES], F32, name="inv_a%d" % k)
-            later(nc.vector.tensor_scalar, out=b[:], in0=v[:], scalar1=-2.0 / m, scalar2=1.0, op0=ALU.mult, op1=ALU.add)
-            later(nc.vector.tensor_scalar_add, out=a[:], in0=b[:], scalar1=1.0)
+            nc.vector.tensor_scalar(out=b[:], in0=v[:], scalar1=-2.0 / m, scalar2=1.0, op0=ALU.mult, op1=ALU.add)
+            nc.vector.tensor_scalar_add(out=a[:], in0=b[:], scalar1=1.0)
             for step in range(T2):
-                later(nc.vector.tensor_mul, out=b[:], in0=b[:], in1=b[:])
-                later(nc.vector.scalar_tensor_tensor, out=a[:], in0=b[:], scalar=1.0, in1=a[:], op0=ALU.add, op1=ALU.mult)
+                nc.vector.tensor_mul(out=b[:], in0=b[:], in1=b[:])
+                nc.vector.scalar_tensor_tensor(out=a[:], in0=b[:], scalar=1.0, in1=a[:], op0=ALU.add, op1=ALU.mult)
             return a
 
         def sum_powers(e, rsum):
@@ -234,30 +231,18 @@ def tile_combnethe_pa_kernel(tc, x, W1o, b1o, W2o, b2o, W1f, b1f, W2f, b2f, out)
             sm = small.tile([P, B_TILES], F32, name="sm%d" % k)
             factor = small.tile([P, B_TILES], F32, name="factor%d" % k)
             if k == 0:
-                later(nc.vector.tensor_scalar_add, out=sm[:], in0=power_sums[k][:], scalar1=tau_power)
+                nc.vector.tensor_scalar_add(out=sm[:], in0=power_sums[k][:], scalar1=tau_power)
                 a = inv_poly(sm, m, k)
-                later(nc.vector.tensor_scalar_mul, out=factor[:], in0=a[:], scalar1=2.0 / m)
+                nc.vector.tensor_scalar_mul(out=factor[:], in0=a[:], scalar1=2.0 / m)
             else:
                 squared_factor = small.tile([P, B_TILES], F32, name="factor_sq%d" % k)
-                later(nc.vector.tensor_mul, out=squared_factor[:], in0=factors[k - 1][:], in1=factors[k - 1][:])
-                later(
-                    nc.vector.scalar_tensor_tensor,
-                    out=sm[:],
-                    in0=power_sums[k][:],
-                    scalar=tau_power,
-                    in1=squared_factor[:],
-                    op0=ALU.add,
-                    op1=ALU.mult,
+                nc.vector.tensor_mul(out=squared_factor[:], in0=factors[k - 1][:], in1=factors[k - 1][:])
+                nc.vector.scalar_tensor_tensor(
+                    out=sm[:], in0=power_sums[k][:], scalar=tau_power, in1=squared_factor[:], op0=ALU.add, op1=ALU.mult
                 )
                 a = inv_poly(sm, m, k)
-                later(
-                    nc.vector.scalar_tensor_tensor,
-                    out=factor[:],
-                    in0=a[:],
-                    scalar=2.0 / m,
-                    in1=squared_factor[:],
-                    op0=ALU.mult,
-                    op1=ALU.mult,
+                nc.vector.scalar_tensor_tensor(
+                    out=factor[:], in0=a[:], scalar=2.0 / m, in1=squared_factor[:], op0=ALU.mult, op1=ALU.mult
                 )
             factors.append(factor)
 
@@ -360,24 +345,18 @@ def tile_combnethe_pa_kernel(tc, x, W1o, b1o, W2o, b2o, W1f, b1f, W2f, b2f, out)
                 regroup_h(s)
             if s == GATE_START:
                 e1, esum1 = softmax_parts(0)
+            if s == GATE_START + 1:
                 rsum1 = small.tile([P, B_TILES], F32)
                 nc.vector.reciprocal(out=rsum1[:], in_=esum1[:])
                 sum_powers(e1, rsum1)
-                for k in range(T1):
-                    gate_round(k)
+            if GATE_START + 2 <= s < GATE_START + 2 + T1:
+                gate_round(s - GATE_START - 2)
+            if s == GATE_START + 2 + T1:
+                cond = small.tile([P, B_TILES], F32)
+                nc.vector.tensor_scalar_mul(out=cond[:], in0=factors[T1 - 1][:], scalar1=TAU ** (2**T1))
                 keep = small.tile([P, B_TILES], F32)
-                later(
-                    nc.vector.tensor_scalar,
-                    out=keep[:],
-                    in0=factors[T1 - 1][:],
-                    scalar1=-TAU_LAST,
-                    scalar2=1.0,
-                    op0=ALU.mult,
-                    op1=ALU.add,
-                )
-                later(nc.vector.tensor_mul, out=keep[:], in0=keep[:], in1=rsum1[:])
-            if s == TOTAL - 1:
-                assert not small_ops
+                nc.vector.tensor_scalar(out=keep[:], in0=cond[:], scalar1=-1.0, scalar2=1.0, op0=ALU.mult, op1=ALU.add)
+                nc.vector.tensor_mul(out=keep[:], in0=keep[:], in1=rsum1[:])
                 share1 = soft.tile([P, B_TILES, C], F32)
                 nc.vector.tensor_tensor(
                     out=share1[:], in0=e1[:], in1=keep[:].unsqueeze(2).to_broadcast([P, B_TILES, C]), op=ALU.mult
@@ -389,14 +368,7 @@ def tile_combnethe_pa_kernel(tc, x, W1o, b1o, W2o, b2o, W1f, b1f, W2f, b2f, out)
         out_tiles = out.rearrange("(i p) c -> i p c", p=P)
         for i in range(B_TILES):
             nc.vector.reciprocal(out=weight2[:, i : i + 1], in_=esum2[:, i : i + 1])
-            nc.vector.scalar_tensor_tensor(
-                out=weight2[:, i : i + 1],
-                in0=weight2[:, i : i + 1],
-                scalar=TAU_LAST,
-                in1=factors[T1 - 1][:, i : i + 1],
-                op0=ALU.mult,
-                op1=ALU.mult,
-            )
+            nc.vector.tensor_mul(out=weight2[:, i : i + 1], in0=weight2[:, i : i + 1], in1=cond[:, i : i + 1])
             nc.vector.scalar_tensor_tensor(
                 out=result[:, i, :],
                 in0=e2[:, i, :],

@@ -25,9 +25,10 @@ TOTAL = NETS * ROUNDS
 B_TILES = B // P
 B1_ROWS = D_H // P
 B2_ROW = NETS * B1_ROWS
-RAW_BUFS = 6
+RAW_BUFS = 8
 LAST_ROUND_PARTS = 2
-W2_AHEAD = 2
+V_COLS = 288
+W2_GROUP = 4
 
 FLOPS = NETS * (2 * B * D_IN * D_H + 2 * B * D_H * C)
 
@@ -39,15 +40,27 @@ def regroup(copy, grouped, planes):
     )
 
 
+def regroup2(copy, grouped, planes):
+    copy(
+        out=grouped.rearrange("p a (c i) j -> p a c j i", i=4),
+        in_=planes.rearrange("p a j (c i) -> p a c j i", i=4),
+    )
+
+
 def tile_combnethe_pa_kernel(tc, x, W1o, b1o, W2o, b2o, W1f, b1f, W2f, b2f, out):
     nc = tc.nc
     W1, b1, W2, b2 = (W1o, W1f), (b1o, b1f), (W2o, W2f), (b2o, b2f)
     with ExitStack() as ctx:
+        ctx.enter_context(
+            tc.manual_schedule(
+                engines={mybir.EngineType.DVE, mybir.EngineType.Activation, mybir.EngineType.PE}
+            )
+        )
         const = ctx.enter_context(tc.tile_pool(name="const", bufs=1))
         w1_raw_pool = ctx.enter_context(tc.tile_pool(name="w1_raw", bufs=RAW_BUFS))
         w1_grp_pool = ctx.enter_context(tc.tile_pool(name="w1_grp", bufs=3))
         w1_mx_pool = ctx.enter_context(tc.tile_pool(name="w1_mx", bufs=3))
-        w2_pool = ctx.enter_context(tc.tile_pool(name="w2", bufs=3))
+        w2_pool = ctx.enter_context(tc.tile_pool(name="w2", bufs=2))
         h_pool = ctx.enter_context(tc.tile_pool(name="h", bufs=3))
         soft = ctx.enter_context(tc.tile_pool(name="soft", bufs=1))
         small = ctx.enter_context(tc.tile_pool(name="small", bufs=1))
@@ -60,23 +73,31 @@ def tile_combnethe_pa_kernel(tc, x, W1o, b1o, W2o, b2o, W1f, b1f, W2f, b2f, out)
         logits = {}
         power_sums, factors = [], []
 
-        def load_w1(r):
+        def load_w1(r, passes=range(IN_PASSES)):
             net, g = divmod(r, ROUNDS)
-            raw = w1_raw_pool.tile([P, IN_PASSES, PACK, K_PASS], BF16, name="w1_raw")
-            for c in range(IN_PASSES):
+            if r not in w1_raw:
+                w1_raw[r] = w1_raw_pool.tile([P, IN_PASSES, PACK, K_PASS], BF16, name="w1_raw")
+            raw = w1_raw[r]
+            for c in passes:
                 nc.sync.dma_start(
                     out=raw[:, c],
                     in_=W1[net][c * K_PASS : (c + 1) * K_PASS, g * K_PASS : (g + 1) * K_PASS].rearrange(
                         "(p j) w -> p j w", j=PACK
                     ),
                 )
-            w1_raw[r] = raw
 
-        def regroup_w1(r):
-            grp = w1_grp_pool.tile([P, IN_PASSES, K_PASS, PACK], BF16, name="w1_grp", align_bytes=64)
-            regroup(nc.vector.tensor_copy, grp[:, 0], w1_raw[r][:, 0])
-            regroup(nc.scalar.copy, grp[:, 1], w1_raw[r][:, 1])
-            w1_grp[r] = grp
+        def w1_grouped(r):
+            if r not in w1_grp:
+                w1_grp[r] = w1_grp_pool.tile([P, IN_PASSES, K_PASS, PACK], BF16, name="w1_grp", align_bytes=64)
+            return w1_grp[r]
+
+        def regroup_w1_vector(r, passes):
+            cols = slice(0, V_COLS)
+            regroup2(nc.vector.tensor_copy, w1_grouped(r)[:, passes, cols], w1_raw[r][:, passes, :, cols])
+
+        def regroup_w1_scalar(r, passes):
+            cols = slice(V_COLS, K_PASS)
+            regroup2(nc.scalar.copy, w1_grouped(r)[:, passes, cols], w1_raw[r][:, passes, :, cols])
 
         def quantise_w1(r):
             codes = w1_mx_pool.tile([P, IN_PASSES, K_PASS], U32, name="w1_codes", align_bytes=64)
@@ -88,26 +109,30 @@ def tile_combnethe_pa_kernel(tc, x, W1o, b1o, W2o, b2o, W1f, b1f, W2f, b2f, out)
             )
             w1_codes[r], w1_scales[r] = codes, scales
 
-        def load_w2(r):
-            net, g = divmod(r, ROUNDS)
-            raw = w2_pool.tile([P, PACK, C], BF16, name="w2_raw")
-            nc.sync.dma_start(
-                out=raw[:], in_=W2[net][g * K_PASS : (g + 1) * K_PASS, :].rearrange("(t p) n -> p t n", p=P)
-            )
-            w2_raw[r] = raw
+        def load_w2(q):
+            net, g = divmod(q * W2_GROUP, ROUNDS)
+            raw = w2_pool.tile([P, PACK, W2_GROUP * C], BF16, name="w2_raw")
+            for k in range(W2_GROUP):
+                rows = slice((g + k) * K_PASS, (g + k + 1) * K_PASS)
+                nc.sync.dma_start(
+                    out=raw[:, :, k * C : (k + 1) * C], in_=W2[net][rows, :].rearrange("(t p) n -> p t n", p=P)
+                )
+            w2_raw[q] = raw
 
-        def regroup_w2(r):
-            grp = w2_pool.tile([P, C, PACK], BF16, name="w2_grp", align_bytes=64)
-            regroup(nc.vector.tensor_copy, grp[:], w2_raw[r][:])
-            w2_grp[r] = grp
+        def regroup_w2(q):
+            grp = w2_pool.tile([P, W2_GROUP * C, PACK], BF16, name="w2_grp", align_bytes=64)
+            regroup(nc.vector.tensor_copy, grp[:], w2_raw[q][:])
+            w2_grp[q] = grp
 
-        def quantise_w2(r):
-            codes = w2_pool.tile([P, C], U32, name="w2_codes", align_bytes=64)
-            scales = w2_pool.tile([P, C], U8, name="w2_scales", align_bytes=64)
+        def quantise_w2(q):
+            codes = w2_pool.tile([P, W2_GROUP, C], U32, name="w2_codes", align_bytes=64)
+            scales = w2_pool.tile([P, W2_GROUP, C], U8, name="w2_scales", align_bytes=64)
             nc.vector.quantize_mx(
-                out=codes[:].bitcast(FP8X4), scales=scales[:], in_=w2_grp[r][:].rearrange("p n t -> p (n t)")
+                out=codes[:].rearrange("p g n -> p (g n)").bitcast(FP8X4),
+                scales=scales[:].rearrange("p g n -> p (g n)"),
+                in_=w2_grp[q][:].rearrange("p w t -> p (w t)"),
             )
-            w2_codes[r], w2_scales[r] = codes, scales
+            w2_codes[q], w2_scales[q] = codes, scales
 
         def batch_parts(r):
             n = LAST_ROUND_PARTS if r == TOTAL - 1 else 1
@@ -173,40 +198,53 @@ def tile_combnethe_pa_kernel(tc, x, W1o, b1o, W2o, b2o, W1f, b1f, W2f, b2f, out)
                     out=logits[i][:],
                     lhsT=h_codes[r][:, rows].bitcast(FP8X4),
                     lhsT_scale=h_scales[r][:, rows],
-                    rhs=w2_codes[r][:].bitcast(FP8X4),
-                    rhs_scale=w2_scales[r][:],
+                    rhs=w2_codes[r // W2_GROUP][:, r % W2_GROUP].bitcast(FP8X4),
+                    rhs_scale=w2_scales[r // W2_GROUP][:, r % W2_GROUP],
                     start=(g == 0),
                     stop=(g == ROUNDS - 1),
                 )
 
-        def softmax_parts(net):
+        def softmax_tiles(net):
             z = soft.tile([P, B_TILES, C], F32, name="z%d" % net)
             negmax = small.tile([P, B_TILES], F32, name="negmax%d" % net)
             e = soft.tile([P, B_TILES, C], F32, name="e%d" % net)
             esum = small.tile([P, B_TILES], F32, name="esum%d" % net)
-            for i in range(B_TILES):
-                nc.vector.tensor_tensor(out=z[:, i, :], in0=logits[i][:], in1=b2_bc[:, net, :], op=ALU.add)
-                nc.vector.tensor_reduce(
-                    out=negmax[:, i : i + 1], in_=z[:, i, :], axis=AX.X, op=ALU.max, negate=True
-                )
-                nc.scalar.activation(
-                    out=e[:, i, :],
-                    in_=z[:, i, :],
-                    func=ACT.Exp,
-                    bias=negmax[:, i : i + 1],
-                    scale=1.0,
-                    accum_out=esum[:, i : i + 1],
-                )
-            return e, esum
+            return z, negmax, e, esum
+
+        def add_b2(net, z, i):
+            nc.vector.tensor_tensor(out=z[:, i, :], in0=logits[i][:], in1=b2_bc[:, net, :], op=ALU.add)
+
+        def row_max(z, negmax, tiles):
+            nc.vector.tensor_reduce(out=negmax[:, tiles], in_=z[:, tiles, :], axis=AX.X, op=ALU.max, negate=True)
+
+        def exponential(z, negmax, e, esum, i):
+            nc.scalar.activation(
+                out=e[:, i, :],
+                in_=z[:, i, :],
+                func=ACT.Exp,
+                bias=negmax[:, i : i + 1],
+                scale=1.0,
+                accum_out=esum[:, i : i + 1],
+            )
+
+        def affine(dst, src, factor, offset):
+            nc.gpsimd.tensor_scalar(
+                out=dst[:], in0=src[:], scalar1=factor, scalar2=offset, op0=ALU.mult, op1=ALU.add
+            )
+
+        def times(dst, first, second):
+            nc.gpsimd.tensor_tensor(out=dst[:], in0=first[:], in1=second[:], op=ALU.mult)
 
         def inv_poly(v, m, k):
             b = small.tile([P, B_TILES], F32, name="inv_b%d" % k)
             a = small.tile([P, B_TILES], F32, name="inv_a%d" % k)
-            nc.vector.tensor_scalar(out=b[:], in0=v[:], scalar1=-2.0 / m, scalar2=1.0, op0=ALU.mult, op1=ALU.add)
-            nc.vector.tensor_scalar_add(out=a[:], in0=b[:], scalar1=1.0)
+            plus = small.tile([P, B_TILES], F32, name="inv_plus%d" % k)
+            affine(b, v, -2.0 / m, 1.0)
+            affine(a, b, 1.0, 1.0)
             for step in range(T2):
-                nc.vector.tensor_mul(out=b[:], in0=b[:], in1=b[:])
-                nc.vector.scalar_tensor_tensor(out=a[:], in0=b[:], scalar=1.0, in1=a[:], op0=ALU.add, op1=ALU.mult)
+                times(b, b, b)
+                affine(plus, b, 1.0, 1.0)
+                times(a, a, plus)
             return a
 
         def sum_powers(e, rsum):
@@ -230,26 +268,24 @@ def tile_combnethe_pa_kernel(tc, x, W1o, b1o, W2o, b2o, W1f, b1f, W2f, b2f, out)
             m = 2.0 + TAU * TAU if k == 0 else 2.0
             sm = small.tile([P, B_TILES], F32, name="sm%d" % k)
             factor = small.tile([P, B_TILES], F32, name="factor%d" % k)
-            if k == 0:
-                nc.vector.tensor_scalar_add(out=sm[:], in0=power_sums[k][:], scalar1=tau_power)
-                a = inv_poly(sm, m, k)
-                nc.vector.tensor_scalar_mul(out=factor[:], in0=a[:], scalar1=2.0 / m)
-            else:
+            affine(sm, power_sums[k], 1.0, tau_power)
+            if k > 0:
                 squared_factor = small.tile([P, B_TILES], F32, name="factor_sq%d" % k)
-                nc.vector.tensor_mul(out=squared_factor[:], in0=factors[k - 1][:], in1=factors[k - 1][:])
-                nc.vector.scalar_tensor_tensor(
-                    out=sm[:], in0=power_sums[k][:], scalar=tau_power, in1=squared_factor[:], op0=ALU.add, op1=ALU.mult
-                )
-                a = inv_poly(sm, m, k)
-                nc.vector.scalar_tensor_tensor(
-                    out=factor[:], in0=a[:], scalar=2.0 / m, in1=squared_factor[:], op0=ALU.mult, op1=ALU.mult
-                )
+                times(squared_factor, factors[k - 1], factors[k - 1])
+                times(sm, sm, squared_factor)
+            a = inv_poly(sm, m, k)
+            affine(factor, a, 2.0 / m, 0.0)
+            if k > 0:
+                times(factor, factor, squared_factor)
             factors.append(factor)
 
         x_sb = const.tile([P, B_TILES, D_IN], BF16)
-        nc.sync.dma_start(out=x_sb[:], in_=x.rearrange("(i p) k -> p i k", p=P))
         bias_rows = const.tile([P, P], BF16)
-        nc.vector.memset(bias_rows[:], 0.0)
+        load_w1(0)
+        for half in range(2):
+            tiles = slice(2 * half, 2 * half + 2)
+            nc.sync.dma_start(out=x_sb[:, tiles], in_=x[half * 2 * P : (half + 1) * 2 * P, :].rearrange("(i p) k -> p i k", p=P))
+        nc.gpsimd.memset(bias_rows[:], 0.0)
         for net in range(NETS):
             nc.sync.dma_start(
                 out=bias_rows[net * B1_ROWS : (net + 1) * B1_ROWS, :], in_=b1[net].rearrange("(r p) -> r p", p=P)
@@ -257,10 +293,13 @@ def tile_combnethe_pa_kernel(tc, x, W1o, b1o, W2o, b2o, W1f, b1f, W2f, b2f, out)
             nc.sync.dma_start(
                 out=bias_rows[B2_ROW + net : B2_ROW + net + 1, :], in_=b2[net].rearrange("(o c) -> o c", o=1)
             )
-        for r in range(RAW_BUFS):
+        load_w1(1)
+        load_w1(2)
+        load_w2(0)
+        load_w1(3)
+        load_w2(1)
+        for r in range(4, RAW_BUFS):
             load_w1(r)
-            if r < W2_AHEAD:
-                load_w2(r)
 
         warm = const.tile([P, 1], F32)
         nc.vector.memset(warm[:], 0.0)
@@ -269,112 +308,138 @@ def tile_combnethe_pa_kernel(tc, x, W1o, b1o, W2o, b2o, W1f, b1f, W2f, b2f, out)
         ident = const.tile([P, P], F32)
         make_identity(nc, ident[:])
 
-        bias_rows_f32 = const.tile([P, P], F32)
-        nc.vector.tensor_copy(out=bias_rows_f32[:], in_=bias_rows[:])
-
         x_words = x_sb[:].bitcast(F32).rearrange("p i (c q u) -> p i c u q", c=IN_PASSES, u=2)
         x_grp = const.tile([P, IN_PASSES, B, PACK], BF16, align_bytes=64)
         x_grp_words = x_grp[:].bitcast(F32)
-        for c in range(IN_PASSES):
-            for half in range(2):
+        x_codes = const.tile([P, IN_PASSES, B], U32, align_bytes=64)
+        x_scales = const.tile([P, IN_PASSES, B], U8, align_bytes=64)
+
+        def transpose_x(half):
+            for c in range(IN_PASSES):
                 xt = psum_h.tile([P, 2, 2 * P], F32, tag="bank")
                 for u in range(2):
                     for ii in range(2):
                         nc.tensor.transpose(
                             out=xt[:, u, ii * P : (ii + 1) * P], in_=x_words[:, 2 * half + ii, c, u, :], identity=ident[:]
                         )
-                copy = nc.vector.tensor_copy if half == 0 else nc.scalar.copy
-                copy(
+                nc.scalar.copy(
                     out=x_grp_words[:, c, half * 2 * P : (half + 1) * 2 * P, :],
                     in_=xt[:].rearrange("p u b -> p b u"),
                 )
 
-        bias_ps = psum_h.tile([P, P], F32, tag="bank")
+        def quantise_x():
+            nc.vector.quantize_mx(
+                out=x_codes[:].rearrange("p c b -> p (c b)").bitcast(FP8X4),
+                scales=x_scales[:].rearrange("p c b -> p (c b)"),
+                in_=x_grp[:].rearrange("p c b t -> p (c b t)"),
+            )
+
+        FIRST, SECOND, BOTH = slice(0, 1), slice(1, 2), slice(0, 2)
+        regroup_w1_vector(0, FIRST)
+        regroup_w1_scalar(0, FIRST)
+        regroup_w1_vector(0, SECOND)
+        regroup_w1_scalar(0, SECOND)
+        transpose_x(0)
+        transpose_x(1)
+        bias_rows_f32 = const.tile([P, P], F32)
+        nc.scalar.copy(out=bias_rows_f32[:], in_=bias_rows[:])
+        bias_ps = psum_l.tile([P, P], F32, name="logits0")
         nc.tensor.transpose(out=bias_ps[:], in_=bias_rows_f32[:], identity=ident[:])
         bias_cols = const.tile([P, P], F32)
-        nc.vector.tensor_copy(out=bias_cols[:], in_=bias_ps[:])
-
-        x_codes = const.tile([P, IN_PASSES, B], U32, align_bytes=64)
-        x_scales = const.tile([P, IN_PASSES, B], U8, align_bytes=64)
-        nc.vector.quantize_mx(
-            out=x_codes[:].rearrange("p c b -> p (c b)").bitcast(FP8X4),
-            scales=x_scales[:].rearrange("p c b -> p (c b)"),
-            in_=x_grp[:].rearrange("p c b t -> p (c b t)"),
-        )
-
-        b2_ps = psum_h.tile([P, NETS, C], F32, tag="bank")
-        for net in range(NETS):
-            nc.tensor.matmul(
-                out=b2_ps[:, net, :],
-                lhsT=bias_cols[:, B2_ROW + net : B2_ROW + net + 1].to_broadcast([P, P]),
-                rhs=ident[:],
-                start=True,
-                stop=True,
-            )
-        b2_bc = const.tile([P, NETS, C], F32)
-        nc.vector.tensor_copy(out=b2_bc[:], in_=b2_ps[:])
-
-        for r in range(2):
-            regroup_w1(r)
-            load_w1(r + RAW_BUFS)
+        nc.scalar.copy(out=bias_cols[:], in_=bias_ps[:])
         quantise_w1(0)
+        regroup_w1_vector(1, FIRST)
+        quantise_x()
         layer1_passes(0)
+        regroup_w1_vector(1, SECOND)
+        regroup_w1_scalar(1, BOTH)
 
-        GATE_START = ROUNDS
-        for s in range(TOTAL + 1):
+        for s in range(TOTAL):
             if s + 1 < TOTAL:
                 quantise_w1(s + 1)
             if s >= 1:
                 quantise_h(s - 1)
-            if s < TOTAL:
-                regroup_w2(s)
-                layer1_exits(s)
+            layer1_exits(s)
+            if s == ROUNDS + 1:
+                z1, negmax1, e1, esum1 = softmax_tiles(0)
+                for i in range(B_TILES):
+                    add_b2(0, z1, i)
+            if s == ROUNDS + 2:
+                for i in range(B_TILES):
+                    exponential(z1, negmax1, e1, esum1, i)
+            if s == ROUNDS + 3:
+                sum_powers(e1, rsum1)
             if s + 2 < TOTAL:
-                regroup_w1(s + 2)
-            if s + W2_AHEAD < TOTAL:
-                load_w2(s + W2_AHEAD)
-            if s + 2 + RAW_BUFS < TOTAL:
-                load_w1(s + 2 + RAW_BUFS)
+                regroup_w1_vector(s + 2, BOTH)
+                regroup_w1_scalar(s + 2, BOTH)
+            if s == 0:
+                regroup_w2(0)
+            elif (s + 2) % W2_GROUP == 0 and s + 2 < TOTAL:
+                regroup_w2((s + 2) // W2_GROUP)
             if s + 1 < TOTAL:
                 layer1_passes(s + 1)
-            if s < TOTAL:
-                quantise_w2(s)
             if s >= 1:
                 layer2(s - 1)
-            if s < TOTAL:
-                regroup_h(s)
-            if s == GATE_START:
-                e1, esum1 = softmax_parts(0)
-            if s == GATE_START + 1:
+            if (s + 1) % W2_GROUP == 0 and s + 1 < TOTAL:
+                quantise_w2((s + 1) // W2_GROUP)
+            regroup_h(s)
+            if s == 0:
+                quantise_w2(0)
+            if (s + 2) % W2_GROUP == 0 and s + 2 + W2_GROUP < TOTAL:
+                load_w2((s + 2) // W2_GROUP + 1)
+            if s + RAW_BUFS < TOTAL:
+                load_w1(s + RAW_BUFS)
+            if s == ROUNDS - 2:
+                b2_ps = psum_h.tile([P, NETS, C], F32, tag="bank")
+                for net in range(NETS):
+                    nc.tensor.matmul(
+                        out=b2_ps[:, net, :],
+                        lhsT=bias_cols[:, B2_ROW + net : B2_ROW + net + 1].to_broadcast([P, P]),
+                        rhs=ident[:],
+                        start=True,
+                        stop=True,
+                    )
+            if s == ROUNDS - 1:
+                b2_bc = const.tile([P, NETS, C], F32)
+                nc.scalar.copy(out=b2_bc[:], in_=b2_ps[:])
+            if s == ROUNDS + 1:
+                row_max(z1, negmax1, slice(0, B_TILES))
+            if s == ROUNDS + 2:
                 rsum1 = small.tile([P, B_TILES], F32)
                 nc.vector.reciprocal(out=rsum1[:], in_=esum1[:])
-                sum_powers(e1, rsum1)
-            if GATE_START + 2 <= s < GATE_START + 2 + T1:
-                gate_round(s - GATE_START - 2)
-            if s == GATE_START + 2 + T1:
+            if s == ROUNDS + 3:
+                for k in range(T1):
+                    gate_round(k)
                 cond = small.tile([P, B_TILES], F32)
-                nc.vector.tensor_scalar_mul(out=cond[:], in0=factors[T1 - 1][:], scalar1=TAU ** (2**T1))
+                affine(cond, factors[T1 - 1], TAU ** (2**T1), 0.0)
                 keep = small.tile([P, B_TILES], F32)
-                nc.vector.tensor_scalar(out=keep[:], in0=cond[:], scalar1=-1.0, scalar2=1.0, op0=ALU.mult, op1=ALU.add)
-                nc.vector.tensor_mul(out=keep[:], in0=keep[:], in1=rsum1[:])
-                share1 = soft.tile([P, B_TILES, C], F32)
-                nc.vector.tensor_tensor(
-                    out=share1[:], in0=e1[:], in1=keep[:].unsqueeze(2).to_broadcast([P, B_TILES, C]), op=ALU.mult
-                )
+                affine(keep, cond, -1.0, 1.0)
+                times(keep, keep, rsum1)
+        quantise_h(TOTAL - 1)
+        layer2(TOTAL - 1)
 
-        e2, esum2 = softmax_parts(1)
+        z2, negmax2, e2, esum2 = softmax_tiles(1)
+        share1 = soft.tile([P, B_TILES, C], F32)
+        for i in range(B_TILES):
+            nc.scalar.activation(out=share1[:, i, :], in_=e1[:, i, :], func=ACT.Copy, scale=keep[:, i : i + 1])
         weight2 = small.tile([P, B_TILES], F32)
         result = soft.tile([P, B_TILES, C], F32)
         out_tiles = out.rearrange("(i p) c -> i p c", p=P)
         for i in range(B_TILES):
-            nc.vector.reciprocal(out=weight2[:, i : i + 1], in_=esum2[:, i : i + 1])
-            nc.vector.tensor_mul(out=weight2[:, i : i + 1], in0=weight2[:, i : i + 1], in1=cond[:, i : i + 1])
-            nc.vector.scalar_tensor_tensor(
-                out=result[:, i, :],
-                in0=e2[:, i, :],
-                scalar=weight2[:, i : i + 1],
-                in1=share1[:, i, :],
-                op0=ALU.mult,
-                op1=ALU.add,
-            )
-            nc.sync.dma_start(out=out_tiles[i], in_=result[:, i, :])
+            add_b2(1, z2, i)
+        for i in range(B_TILES):
+            row_max(z2, negmax2, slice(i, i + 1))
+            exponential(z2, negmax2, e2, esum2, i)
+        for pair in (slice(0, 2), slice(2, 4)):
+            nc.vector.reciprocal(out=weight2[:, pair], in_=esum2[:, pair])
+            nc.vector.tensor_mul(out=weight2[:, pair], in0=weight2[:, pair], in1=cond[:, pair])
+            for i in range(pair.start, pair.stop):
+                nc.vector.scalar_tensor_tensor(
+                    out=result[:, i, :],
+                    in0=e2[:, i, :],
+                    scalar=weight2[:, i : i + 1],
+                    in1=share1[:, i, :],
+                    op0=ALU.mult,
+                    op1=ALU.add,
+                )
+                nc.sync.dma_start(out=out_tiles[i], in_=result[:, i, :])

@@ -1,4 +1,5 @@
 from contextlib import ExitStack
+from functools import partial
 
 import concourse.mybir as mybir
 from concourse.masks import make_identity
@@ -27,7 +28,7 @@ B1_ROWS = D_H // P
 B2_ROW = NETS * B1_ROWS
 RAW_BUFS = 8
 LAST_ROUND_PARTS = 2
-V_COLS = 288
+V_COLS = 272
 W2_GROUP = 4
 
 FLOPS = NETS * (2 * B * D_IN * D_H + 2 * B * D_H * C)
@@ -71,7 +72,7 @@ def tile_combnethe_pa_kernel(tc, x, W1o, b1o, W2o, b2o, W1f, b1f, W2f, b2f, out)
         w2_raw, w2_grp, w2_codes, w2_scales = {}, {}, {}, {}
         h_banks, h_planes, h_grp, h_codes, h_scales = {}, {}, {}, {}, {}
         logits = {}
-        power_sums, factors = [], []
+        gate_queue = []
 
         def load_w1(r, passes=range(IN_PASSES)):
             net, g = divmod(r, ROUNDS)
@@ -86,17 +87,27 @@ def tile_combnethe_pa_kernel(tc, x, W1o, b1o, W2o, b2o, W1f, b1f, W2f, b2f, out)
                     ),
                 )
 
+        def load_w1_halves(r):
+            net, g = divmod(r, ROUNDS)
+            w1_raw[r] = w1_raw_pool.tile([P, IN_PASSES, PACK, K_PASS], BF16, name="w1_raw")
+            for c in range(IN_PASSES):
+                for k in range(2):
+                    half = slice(k * K_PASS // 2, (k + 1) * K_PASS // 2)
+                    cols = slice(g * K_PASS + half.start, g * K_PASS + half.stop)
+                    nc.sync.dma_start(
+                        out=w1_raw[r][:, c, :, half],
+                        in_=W1[net][c * K_PASS : (c + 1) * K_PASS, cols].rearrange("(p j) w -> p j w", j=PACK),
+                    )
+
         def w1_grouped(r):
             if r not in w1_grp:
                 w1_grp[r] = w1_grp_pool.tile([P, IN_PASSES, K_PASS, PACK], BF16, name="w1_grp", align_bytes=64)
             return w1_grp[r]
 
-        def regroup_w1_vector(r, passes):
-            cols = slice(0, V_COLS)
+        def regroup_w1_vector(r, passes, cols=slice(0, V_COLS)):
             regroup2(nc.vector.tensor_copy, w1_grouped(r)[:, passes, cols], w1_raw[r][:, passes, :, cols])
 
-        def regroup_w1_scalar(r, passes):
-            cols = slice(V_COLS, K_PASS)
+        def regroup_w1_scalar(r, passes, cols=slice(V_COLS, K_PASS)):
             regroup2(nc.scalar.copy, w1_grouped(r)[:, passes, cols], w1_raw[r][:, passes, :, cols])
 
         def quantise_w1(r):
@@ -170,26 +181,26 @@ def tile_combnethe_pa_kernel(tc, x, W1o, b1o, W2o, b2o, W1f, b1f, W2f, b2f, out)
                     )
             h_planes[r] = planes
 
-        def regroup_h(r):
-            grp = h_pool.tile([P, B, PACK], BF16, name="h_grp", align_bytes=64)
-            for rows in batch_parts(r):
-                regroup(nc.vector.tensor_copy, grp[:, rows, :], h_planes[r][:, :, rows])
-            h_grp[r] = grp
+        def h_grouped(r):
+            if r not in h_grp:
+                h_grp[r] = h_pool.tile([P, B, PACK], BF16, name="h_grp", align_bytes=64)
+                h_codes[r] = h_pool.tile([P, B], U32, name="h_codes", align_bytes=64)
+                h_scales[r] = h_pool.tile([P, B], U8, name="h_scales", align_bytes=64)
+            return h_grp[r]
 
-        def quantise_h(r):
-            codes = h_pool.tile([P, B], U32, name="h_codes", align_bytes=64)
-            scales = h_pool.tile([P, B], U8, name="h_scales", align_bytes=64)
-            for rows in batch_parts(r):
-                nc.vector.quantize_mx(
-                    out=codes[:, rows].bitcast(FP8X4),
-                    scales=scales[:, rows],
-                    in_=h_grp[r][:, rows, :].rearrange("p b t -> p (b t)"),
-                )
-            h_codes[r], h_scales[r] = codes, scales
+        def regroup_h(r, rows):
+            regroup(nc.vector.tensor_copy, h_grouped(r)[:, rows, :], h_planes[r][:, :, rows])
 
-        def layer2(r):
+        def quantise_h(r, rows):
+            nc.vector.quantize_mx(
+                out=h_codes[r][:, rows].bitcast(FP8X4),
+                scales=h_scales[r][:, rows],
+                in_=h_grp[r][:, rows, :].rearrange("p b t -> p (b t)"),
+            )
+
+        def layer2(r, tiles=range(B_TILES)):
             net, g = divmod(r, ROUNDS)
-            for i in range(B_TILES):
+            for i in tiles:
                 if g == 0:
                     bank = psum_l.tile([P, C], F32, name="logits%d" % i)
                     logits[i] = bank
@@ -227,61 +238,79 @@ def tile_combnethe_pa_kernel(tc, x, W1o, b1o, W2o, b2o, W1f, b1f, W2f, b2f, out)
                 accum_out=esum[:, i : i + 1],
             )
 
-        def affine(dst, src, factor, offset):
-            nc.gpsimd.tensor_scalar(
-                out=dst[:], in0=src[:], scalar1=factor, scalar2=offset, op0=ALU.mult, op1=ALU.add
-            )
+        def sum_power(k, e, rsum):
+            squared = soft.tile([P, B_TILES, C], F32, name="power%d" % k)
+            for i in range(B_TILES):
+                nc.scalar.activation(
+                    out=squared[:, i, :],
+                    in_=e[:, i, :],
+                    func=ACT.Square,
+                    scale=(rsum[:, i : i + 1] if k == 0 else 1.0),
+                    accum_out=power_sums[:, k, i : i + 1],
+                )
+            return squared
 
-        def times(dst, first, second):
-            nc.gpsimd.tensor_tensor(out=dst[:], in0=first[:], in1=second[:], op=ALU.mult)
+        def gate_stages():
+            v = nc.vector
+            stages = []
 
-        def inv_poly(v, m, k):
-            b = small.tile([P, B_TILES], F32, name="inv_b%d" % k)
-            a = small.tile([P, B_TILES], F32, name="inv_a%d" % k)
-            plus = small.tile([P, B_TILES], F32, name="inv_plus%d" % k)
-            affine(b, v, -2.0 / m, 1.0)
-            affine(a, b, 1.0, 1.0)
-            for step in range(T2):
-                times(b, b, b)
-                affine(plus, b, 1.0, 1.0)
-                times(a, a, plus)
-            return a
+            def stage(*calls):
+                stages.append(calls)
 
-        def sum_powers(e, rsum):
-            power = e
             for k in range(T1):
-                squared = soft.tile([P, B_TILES, C], F32, name="power%d" % k)
-                total = small.tile([P, B_TILES], F32, name="power_sum%d" % k)
-                for i in range(B_TILES):
-                    nc.scalar.activation(
-                        out=squared[:, i, :],
-                        in_=power[:, i, :],
-                        func=ACT.Square,
-                        scale=(rsum[:, i : i + 1] if k == 0 else 1.0),
-                        accum_out=total[:, i : i + 1],
+                m = 2.0 + TAU * TAU if k == 0 else 2.0
+                u, r = gate_u[:, k], gate_r[:, k]
+                shift = partial(v.tensor_scalar_add, out=u, in0=power_sums[:, k], scalar1=TAU ** (2 ** (k + 1)))
+                if k == 0:
+                    stage(shift)
+                    row_sum = u
+                else:
+                    stage(shift, partial(v.tensor_mul, out=gate_t[:], in0=gate_f[:], in1=gate_f[:]))
+                    stage(partial(v.tensor_mul, out=gate_t[:], in0=gate_t[:], in1=u))
+                    row_sum = gate_t[:]
+                stage(
+                    partial(
+                        v.tensor_scalar,
+                        out=gate_b[:],
+                        in0=row_sum,
+                        scalar1=-2.0 / m,
+                        scalar2=1.0,
+                        op0=ALU.mult,
+                        op1=ALU.add,
+                    ),
+                    partial(v.reciprocal, out=r, in_=u),
+                )
+                for step in range(T2 + 1):
+                    stage(partial(v.tensor_mul, out=gate_b[:], in0=gate_b[:], in1=gate_b[:]))
+                stage(
+                    partial(
+                        v.scalar_tensor_tensor,
+                        out=gate_f[:],
+                        in0=gate_b[:],
+                        scalar=1.0,
+                        in1=r,
+                        op0=ALU.subtract,
+                        op1=ALU.mult,
                     )
-                power = squared
-                power_sums.append(total)
+                )
+            tau_end = TAU ** (2**T1)
+            stage(
+                partial(v.tensor_scalar_mul, out=cond[:], in0=gate_f[:], scalar1=-tau_end),
+                partial(
+                    v.tensor_scalar, out=keep[:], in0=gate_f[:], scalar1=tau_end, scalar2=1.0, op0=ALU.mult, op1=ALU.add
+                ),
+            )
+            stage(partial(v.tensor_mul, out=keep[:], in0=keep[:], in1=rsum1[:]))
+            return stages
 
-        def gate_round(k):
-            tau_power = TAU ** (2 ** (k + 1))
-            m = 2.0 + TAU * TAU if k == 0 else 2.0
-            sm = small.tile([P, B_TILES], F32, name="sm%d" % k)
-            factor = small.tile([P, B_TILES], F32, name="factor%d" % k)
-            affine(sm, power_sums[k], 1.0, tau_power)
-            if k > 0:
-                squared_factor = small.tile([P, B_TILES], F32, name="factor_sq%d" % k)
-                times(squared_factor, factors[k - 1], factors[k - 1])
-                times(sm, sm, squared_factor)
-            a = inv_poly(sm, m, k)
-            affine(factor, a, 2.0 / m, 0.0)
-            if k > 0:
-                times(factor, factor, squared_factor)
-            factors.append(factor)
+        def fill(count=1):
+            for step in range(min(count, len(gate_queue))):
+                for call in gate_queue.pop(0):
+                    call()
 
         x_sb = const.tile([P, B_TILES, D_IN], BF16)
         bias_rows = const.tile([P, P], BF16)
-        load_w1(0)
+        load_w1_halves(0)
         for half in range(2):
             tiles = slice(2 * half, 2 * half + 2)
             nc.sync.dma_start(out=x_sb[:, tiles], in_=x[half * 2 * P : (half + 1) * 2 * P, :].rearrange("(i p) k -> p i k", p=P))
@@ -300,6 +329,16 @@ def tile_combnethe_pa_kernel(tc, x, W1o, b1o, W2o, b2o, W1f, b1f, W2f, b2f, out)
         load_w2(1)
         for r in range(4, RAW_BUFS):
             load_w1(r)
+
+        power_sums = small.tile([P, T1, B_TILES], F32)
+        gate_u = small.tile([P, T1, B_TILES], F32)
+        gate_r = small.tile([P, T1, B_TILES], F32)
+        gate_t = small.tile([P, B_TILES], F32)
+        gate_b = small.tile([P, B_TILES], F32)
+        gate_f = small.tile([P, B_TILES], F32)
+        cond = small.tile([P, B_TILES], F32)
+        keep = small.tile([P, B_TILES], F32)
+        rsum1 = small.tile([P, B_TILES], F32)
 
         warm = const.tile([P, 1], F32)
         nc.vector.memset(warm[:], 0.0)
@@ -335,10 +374,13 @@ def tile_combnethe_pa_kernel(tc, x, W1o, b1o, W2o, b2o, W1f, b1f, W2f, b2f, out)
             )
 
         FIRST, SECOND, BOTH = slice(0, 1), slice(1, 2), slice(0, 2)
-        regroup_w1_vector(0, FIRST)
-        regroup_w1_scalar(0, FIRST)
-        regroup_w1_vector(0, SECOND)
-        regroup_w1_scalar(0, SECOND)
+        L, R = slice(0, 256), slice(256, 512)
+        regroup_w1_vector(0, FIRST, L)
+        regroup_w1_scalar(0, FIRST, R)
+        regroup_w1_vector(0, SECOND, L)
+        regroup_w1_vector(0, SECOND, slice(256, 384))
+        regroup_w1_scalar(0, SECOND, slice(384, 512))
+        quantise_w1(0)
         transpose_x(0)
         transpose_x(1)
         bias_rows_f32 = const.tile([P, P], F32)
@@ -347,42 +389,56 @@ def tile_combnethe_pa_kernel(tc, x, W1o, b1o, W2o, b2o, W1f, b1f, W2f, b2f, out)
         nc.tensor.transpose(out=bias_ps[:], in_=bias_rows_f32[:], identity=ident[:])
         bias_cols = const.tile([P, P], F32)
         nc.scalar.copy(out=bias_cols[:], in_=bias_ps[:])
-        quantise_w1(0)
-        regroup_w1_vector(1, FIRST)
+        regroup_w1_vector(1, FIRST, slice(0,384))
         quantise_x()
         layer1_passes(0)
-        regroup_w1_vector(1, SECOND)
-        regroup_w1_scalar(1, BOTH)
+        regroup_w1_vector(1, SECOND, slice(0,384))
+        regroup_w1_scalar(1, BOTH, slice(384,512))
 
+        WHOLE = slice(0, B)
         for s in range(TOTAL):
-            if s + 1 < TOTAL:
-                quantise_w1(s + 1)
-            if s >= 1:
-                quantise_h(s - 1)
-            layer1_exits(s)
             if s == ROUNDS + 1:
                 z1, negmax1, e1, esum1 = softmax_tiles(0)
                 for i in range(B_TILES):
                     add_b2(0, z1, i)
+            if s + 1 < TOTAL:
+                quantise_w1(s + 1)
+                fill()
             if s == ROUNDS + 2:
-                for i in range(B_TILES):
-                    exponential(z1, negmax1, e1, esum1, i)
-            if s == ROUNDS + 3:
-                sum_powers(e1, rsum1)
+                nc.vector.reciprocal(out=rsum1[:], in_=esum1[:])
+            if s == ROUNDS + 1:
+                row_max(z1, negmax1, slice(0, B_TILES))
+            if s >= 1 and s < TOTAL - 1:
+                quantise_h(s - 1, WHOLE)
+                fill()
+            layer1_exits(s)
+            if ROUNDS + 2 <= s < ROUNDS + 2 + T1:
+                power = sum_power(s - ROUNDS - 2, e1 if s == ROUNDS + 2 else power, rsum1)
+            if s == ROUNDS + 2:
+                gate_queue.extend(gate_stages())
             if s + 2 < TOTAL:
                 regroup_w1_vector(s + 2, BOTH)
+                if s > ROUNDS + 2:
+                    fill()
                 regroup_w1_scalar(s + 2, BOTH)
+            if s == ROUNDS + 1:
+                for i in range(B_TILES):
+                    exponential(z1, negmax1, e1, esum1, i)
             if s == 0:
                 regroup_w2(0)
             elif (s + 2) % W2_GROUP == 0 and s + 2 < TOTAL:
                 regroup_w2((s + 2) // W2_GROUP)
+                fill()
             if s + 1 < TOTAL:
                 layer1_passes(s + 1)
-            if s >= 1:
+            if s >= 1 and s < TOTAL - 1:
                 layer2(s - 1)
             if (s + 1) % W2_GROUP == 0 and s + 1 < TOTAL:
                 quantise_w2((s + 1) // W2_GROUP)
-            regroup_h(s)
+                fill()
+            if s < TOTAL - 1:
+                regroup_h(s, WHOLE)
+                fill(1 if s < ROUNDS + 3 else 2)
             if s == 0:
                 quantise_w2(0)
             if (s + 2) % W2_GROUP == 0 and s + 2 + W2_GROUP < TOTAL:
@@ -402,41 +458,47 @@ def tile_combnethe_pa_kernel(tc, x, W1o, b1o, W2o, b2o, W1f, b1f, W2f, b2f, out)
             if s == ROUNDS - 1:
                 b2_bc = const.tile([P, NETS, C], F32)
                 nc.scalar.copy(out=b2_bc[:], in_=b2_ps[:])
-            if s == ROUNDS + 1:
-                row_max(z1, negmax1, slice(0, B_TILES))
-            if s == ROUNDS + 2:
-                rsum1 = small.tile([P, B_TILES], F32)
-                nc.vector.reciprocal(out=rsum1[:], in_=esum1[:])
-            if s == ROUNDS + 3:
-                for k in range(T1):
-                    gate_round(k)
-                cond = small.tile([P, B_TILES], F32)
-                affine(cond, factors[T1 - 1], TAU ** (2**T1), 0.0)
-                keep = small.tile([P, B_TILES], F32)
-                affine(keep, cond, -1.0, 1.0)
-                times(keep, keep, rsum1)
-        quantise_h(TOTAL - 1)
-        layer2(TOTAL - 1)
 
         z2, negmax2, e2, esum2 = softmax_tiles(1)
-        share1 = soft.tile([P, B_TILES, C], F32)
-        for i in range(B_TILES):
-            nc.scalar.activation(out=share1[:, i, :], in_=e1[:, i, :], func=ACT.Copy, scale=keep[:, i : i + 1])
         weight2 = small.tile([P, B_TILES], F32)
         result = soft.tile([P, B_TILES, C], F32)
         out_tiles = out.rearrange("(i p) c -> i p c", p=P)
+        last = TOTAL - 1
+        early, late = batch_parts(last)
+        early_tiles, late_tiles = slice(0, B_TILES // 2), slice(B_TILES // 2, B_TILES)
+        regroup_h(last, early)
+        fill()
+        quantise_h(last - 1, WHOLE)
+        fill()
+        layer2(last - 1)
+        quantise_h(last, early)
+        fill()
+        layer2(last, range(0, B_TILES // 2))
+        regroup_h(last, late)
+        fill(len(gate_queue))
+        share1 = soft.tile([P, B_TILES, C], F32)
         for i in range(B_TILES):
+            nc.scalar.activation(out=share1[:, i, :], in_=e1[:, i, :], func=ACT.Copy, scale=keep[:, i : i + 1])
+        quantise_h(last, late)
+        for i in range(0, B_TILES // 2):
             add_b2(1, z2, i)
-        for i in range(B_TILES):
-            row_max(z2, negmax2, slice(i, i + 1))
+        layer2(last, range(B_TILES // 2, B_TILES))
+        row_max(z2, negmax2, early_tiles)
+        for i in range(B_TILES // 2, B_TILES):
+            add_b2(1, z2, i)
+        for i in range(0, B_TILES // 2):
             exponential(z2, negmax2, e2, esum2, i)
-        for pair in (slice(0, 2), slice(2, 4)):
+        row_max(z2, negmax2, late_tiles)
+        for i in range(B_TILES // 2, B_TILES):
+            exponential(z2, negmax2, e2, esum2, i)
+        for pair in (early_tiles, late_tiles):
             nc.vector.reciprocal(out=weight2[:, pair], in_=esum2[:, pair])
-            nc.vector.tensor_mul(out=weight2[:, pair], in0=weight2[:, pair], in1=cond[:, pair])
+            for i in range(pair.start, pair.stop):
+                nc.vector.tensor_scalar_mul(out=z2[:, i, :], in0=e2[:, i, :], scalar1=cond[:, i : i + 1])
             for i in range(pair.start, pair.stop):
                 nc.vector.scalar_tensor_tensor(
                     out=result[:, i, :],
-                    in0=e2[:, i, :],
+                    in0=z2[:, i, :],
                     scalar=weight2[:, i : i + 1],
                     in1=share1[:, i, :],
                     op0=ALU.mult,

@@ -27,8 +27,9 @@ B_TILES = B // P
 B1_ROWS = D_H // P
 B2_ROW = NETS * B1_ROWS
 RAW_BUFS = 8
+ROUTE_COLS = 256
 LAST_ROUND_PARTS = 2
-V_COLS = 272
+V_COLS = 456
 W2_GROUP = 4
 
 FLOPS = NETS * (2 * B * D_IN * D_H + 2 * B * D_H * C)
@@ -65,7 +66,8 @@ def tile_combnethe_pa_kernel(tc, x, W1o, b1o, W2o, b2o, W1f, b1f, W2f, b2f, out)
         h_pool = ctx.enter_context(tc.tile_pool(name="h", bufs=3))
         soft = ctx.enter_context(tc.tile_pool(name="soft", bufs=1))
         small = ctx.enter_context(tc.tile_pool(name="small", bufs=1))
-        psum_h = ctx.enter_context(tc.psum_pool(name="psum_h", bufs=4))
+        psum_h = ctx.enter_context(tc.psum_pool(name="psum_h", bufs=3))
+        psum_r = ctx.enter_context(tc.psum_pool(name="psum_r", bufs=1))
         psum_l = ctx.enter_context(tc.psum_pool(name="psum_l", bufs=1))
 
         w1_raw, w1_grp, w1_codes, w1_scales = {}, {}, {}, {}
@@ -73,6 +75,7 @@ def tile_combnethe_pa_kernel(tc, x, W1o, b1o, W2o, b2o, W1f, b1f, W2f, b2f, out)
         h_banks, h_planes, h_grp, h_codes, h_scales = {}, {}, {}, {}, {}
         logits = {}
         gate_queue = []
+        route = {}
 
         def load_w1(r, passes=range(IN_PASSES)):
             net, g = divmod(r, ROUNDS)
@@ -109,6 +112,25 @@ def tile_combnethe_pa_kernel(tc, x, W1o, b1o, W2o, b2o, W1f, b1f, W2f, b2f, out)
 
         def regroup_w1_scalar(r, passes, cols=slice(V_COLS, K_PASS)):
             regroup2(nc.scalar.copy, w1_grouped(r)[:, passes, cols], w1_raw[r][:, passes, :, cols])
+
+        def shuffle_w1(r, c, cols):
+            bank = psum_r.tile([P, ROUTE_COLS * PACK], BF16, name="route")
+            for first in range(cols.start, cols.stop, P):
+                to = (first - cols.start) * PACK
+                nc.tensor.matmul(
+                    out=bank[:, to : to + P * PACK],
+                    lhsT=ident_bf[:],
+                    rhs=w1_raw[r][:, c, :, first : first + P].rearrange("p j w -> p w j"),
+                    start=True,
+                    stop=True,
+                )
+            route[r] = bank
+
+        def unload_w1(r, c, cols):
+            nc.scalar.copy(
+                out=w1_grouped(r)[:, c, cols].rearrange("p w j -> p (w j)"),
+                in_=route[r][:, 0 : (cols.stop - cols.start) * PACK],
+            )
 
         def quantise_w1(r):
             codes = w1_mx_pool.tile([P, IN_PASSES, K_PASS], U32, name="w1_codes", align_bytes=64)
@@ -149,10 +171,10 @@ def tile_combnethe_pa_kernel(tc, x, W1o, b1o, W2o, b2o, W1f, b1f, W2f, b2f, out)
             n = LAST_ROUND_PARTS if r == TOTAL - 1 else 1
             return [slice(k * B // n, (k + 1) * B // n) for k in range(n)]
 
-        def layer1_passes(r):
-            h_banks[r] = []
-            for rows in batch_parts(r):
-                for t in range(PACK):
+        def layer1_passes(r, ts, parts=(0,)):
+            for part in parts:
+                rows = batch_parts(r)[part]
+                for t in ts:
                     units = slice(t * P, (t + 1) * P)
                     acc = psum_h.tile([P, B // len(batch_parts(r))], F32, tag="bank")
                     for c in range(IN_PASSES):
@@ -165,21 +187,21 @@ def tile_combnethe_pa_kernel(tc, x, W1o, b1o, W2o, b2o, W1f, b1f, W2f, b2f, out)
                             start=(c == 0),
                             stop=(c == IN_PASSES - 1),
                         )
-                    h_banks[r].append(acc)
+                    h_banks[r, part, t] = acc
 
-        def layer1_exits(r):
-            planes = h_pool.tile([P, PACK, B], BF16, name="h_planes")
-            for k, rows in enumerate(batch_parts(r)):
-                for t in range(PACK):
+        def layer1_exits(r, ts, parts=(0,)):
+            if r not in h_planes:
+                h_planes[r] = h_pool.tile([P, PACK, B], BF16, name="h_planes")
+            for part in parts:
+                for t in ts:
                     col = r * PACK + t
                     nc.scalar.activation(
-                        out=planes[:, t, rows],
-                        in_=h_banks[r][k * PACK + t][:],
+                        out=h_planes[r][:, t, batch_parts(r)[part]],
+                        in_=h_banks[r, part, t][:],
                         func=ACT.Relu,
                         bias=bias_cols[:, col : col + 1],
                         scale=1.0,
                     )
-            h_planes[r] = planes
 
         def h_grouped(r):
             if r not in h_grp:
@@ -346,6 +368,8 @@ def tile_combnethe_pa_kernel(tc, x, W1o, b1o, W2o, b2o, W1f, b1f, W2f, b2f, out)
 
         ident = const.tile([P, P], F32)
         make_identity(nc, ident[:])
+        ident_bf = const.tile([P, P], BF16)
+        make_identity(nc, ident_bf[:])
 
         x_words = x_sb[:].bitcast(F32).rearrange("p i (c q u) -> p i c u q", c=IN_PASSES, u=2)
         x_grp = const.tile([P, IN_PASSES, B, PACK], BF16, align_bytes=64)
@@ -375,6 +399,7 @@ def tile_combnethe_pa_kernel(tc, x, W1o, b1o, W2o, b2o, W1f, b1f, W2f, b2f, out)
 
         FIRST, SECOND, BOTH = slice(0, 1), slice(1, 2), slice(0, 2)
         L, R = slice(0, 256), slice(256, 512)
+        FIRST, SECOND, BOTH = slice(0, 1), slice(1, 2), slice(0, 2)
         regroup_w1_vector(0, FIRST, L)
         regroup_w1_scalar(0, FIRST, R)
         regroup_w1_vector(0, SECOND, L)
@@ -389,12 +414,24 @@ def tile_combnethe_pa_kernel(tc, x, W1o, b1o, W2o, b2o, W1f, b1f, W2f, b2f, out)
         nc.tensor.transpose(out=bias_ps[:], in_=bias_rows_f32[:], identity=ident[:])
         bias_cols = const.tile([P, P], F32)
         nc.scalar.copy(out=bias_cols[:], in_=bias_ps[:])
+        b2_ps = psum_l.tile([P, NETS, C], F32, name="logits1")
+        for net in range(NETS):
+            nc.tensor.matmul(
+                out=b2_ps[:, net, :],
+                lhsT=bias_cols[:, B2_ROW + net : B2_ROW + net + 1].to_broadcast([P, P]),
+                rhs=ident[:],
+                start=True,
+                stop=True,
+            )
         regroup_w1_vector(1, FIRST, slice(0,384))
         quantise_x()
-        layer1_passes(0)
+        layer1_passes(0, [0, 1, 2])
         regroup_w1_vector(1, SECOND, slice(0,384))
         regroup_w1_scalar(1, BOTH, slice(384,512))
 
+        b2_bc = const.tile([P, NETS, C], F32)
+        nc.scalar.copy(out=b2_bc[:], in_=b2_ps[:])
+        LEFT = slice(0, ROUTE_COLS)
         WHOLE = slice(0, B)
         for s in range(TOTAL):
             if s == ROUNDS + 1:
@@ -411,16 +448,25 @@ def tile_combnethe_pa_kernel(tc, x, W1o, b1o, W2o, b2o, W1f, b1f, W2f, b2f, out)
             if s >= 1 and s < TOTAL - 1:
                 quantise_h(s - 1, WHOLE)
                 fill()
-            layer1_exits(s)
+            follow = (s + 1, 0) if s + 1 < TOTAL else (s, 1)
+            layer1_exits(s, [0])
+            layer1_passes(s, [3])
+            if s + 2 < TOTAL:
+                shuffle_w1(s + 2, 1, LEFT)
+            for t in range(3):
+                layer1_exits(s, [t + 1])
+                layer1_passes(follow[0], [t], [follow[1]])
             if ROUNDS + 2 <= s < ROUNDS + 2 + T1:
                 power = sum_power(s - ROUNDS - 2, e1 if s == ROUNDS + 2 else power, rsum1)
             if s == ROUNDS + 2:
                 gate_queue.extend(gate_stages())
             if s + 2 < TOTAL:
-                regroup_w1_vector(s + 2, BOTH)
+                regroup_w1_vector(s + 2, FIRST, slice(0, V_COLS))
                 if s > ROUNDS + 2:
                     fill()
-                regroup_w1_scalar(s + 2, BOTH)
+                regroup_w1_scalar(s + 2, SECOND, slice(ROUTE_COLS, K_PASS))
+                regroup_w1_scalar(s + 2, FIRST, slice(V_COLS, K_PASS))
+                unload_w1(s + 2, 1, LEFT)
             if s == ROUNDS + 1:
                 for i in range(B_TILES):
                     exponential(z1, negmax1, e1, esum1, i)
@@ -429,8 +475,6 @@ def tile_combnethe_pa_kernel(tc, x, W1o, b1o, W2o, b2o, W1f, b1f, W2f, b2f, out)
             elif (s + 2) % W2_GROUP == 0 and s + 2 < TOTAL:
                 regroup_w2((s + 2) // W2_GROUP)
                 fill()
-            if s + 1 < TOTAL:
-                layer1_passes(s + 1)
             if s >= 1 and s < TOTAL - 1:
                 layer2(s - 1)
             if (s + 1) % W2_GROUP == 0 and s + 1 < TOTAL:
@@ -445,19 +489,6 @@ def tile_combnethe_pa_kernel(tc, x, W1o, b1o, W2o, b2o, W1f, b1f, W2f, b2f, out)
                 load_w2((s + 2) // W2_GROUP + 1)
             if s + RAW_BUFS < TOTAL:
                 load_w1(s + RAW_BUFS)
-            if s == ROUNDS - 2:
-                b2_ps = psum_h.tile([P, NETS, C], F32, tag="bank")
-                for net in range(NETS):
-                    nc.tensor.matmul(
-                        out=b2_ps[:, net, :],
-                        lhsT=bias_cols[:, B2_ROW + net : B2_ROW + net + 1].to_broadcast([P, P]),
-                        rhs=ident[:],
-                        start=True,
-                        stop=True,
-                    )
-            if s == ROUNDS - 1:
-                b2_bc = const.tile([P, NETS, C], F32)
-                nc.scalar.copy(out=b2_bc[:], in_=b2_ps[:])
 
         z2, negmax2, e2, esum2 = softmax_tiles(1)
         weight2 = small.tile([P, B_TILES], F32)
@@ -465,6 +496,9 @@ def tile_combnethe_pa_kernel(tc, x, W1o, b1o, W2o, b2o, W1f, b1f, W2f, b2f, out)
         out_tiles = out.rearrange("(i p) c -> i p c", p=P)
         last = TOTAL - 1
         early, late = batch_parts(last)
+        layer1_exits(last, [0], [1])
+        layer1_passes(last, [3], [1])
+        layer1_exits(last, [1, 2, 3], [1])
         early_tiles, late_tiles = slice(0, B_TILES // 2), slice(B_TILES // 2, B_TILES)
         regroup_h(last, early)
         fill()

@@ -29,7 +29,7 @@ B2_ROW = NETS * B1_ROWS
 RAW_BUFS = 8
 ROUTE_COLS = 256
 LAST_ROUND_PARTS = 2
-V_COLS = 456
+V_COLS = 448
 W2_GROUP = 4
 
 FLOPS = NETS * (2 * B * D_IN * D_H + 2 * B * D_H * C)
@@ -66,8 +66,7 @@ def tile_combnethe_pa_kernel(tc, x, W1o, b1o, W2o, b2o, W1f, b1f, W2f, b2f, out)
         h_pool = ctx.enter_context(tc.tile_pool(name="h", bufs=3))
         soft = ctx.enter_context(tc.tile_pool(name="soft", bufs=1))
         small = ctx.enter_context(tc.tile_pool(name="small", bufs=1))
-        psum_h = ctx.enter_context(tc.psum_pool(name="psum_h", bufs=3))
-        psum_r = ctx.enter_context(tc.psum_pool(name="psum_r", bufs=1))
+        psum_h = ctx.enter_context(tc.psum_pool(name="psum_h", bufs=4))
         psum_l = ctx.enter_context(tc.psum_pool(name="psum_l", bufs=1))
 
         w1_raw, w1_grp, w1_codes, w1_scales = {}, {}, {}, {}
@@ -114,7 +113,7 @@ def tile_combnethe_pa_kernel(tc, x, W1o, b1o, W2o, b2o, W1f, b1f, W2f, b2f, out)
             regroup2(nc.scalar.copy, w1_grouped(r)[:, passes, cols], w1_raw[r][:, passes, :, cols])
 
         def shuffle_w1(r, c, cols):
-            bank = psum_r.tile([P, ROUTE_COLS * PACK], BF16, name="route")
+            bank = psum_h.tile([P, ROUTE_COLS * PACK], BF16, tag="bank")
             for first in range(cols.start, cols.stop, P):
                 to = (first - cols.start) * PACK
                 nc.tensor.matmul(
@@ -425,7 +424,7 @@ def tile_combnethe_pa_kernel(tc, x, W1o, b1o, W2o, b2o, W1f, b1f, W2f, b2f, out)
             )
         regroup_w1_vector(1, FIRST, slice(0,384))
         quantise_x()
-        layer1_passes(0, [0, 1, 2])
+        layer1_passes(0, range(PACK))
         regroup_w1_vector(1, SECOND, slice(0,384))
         regroup_w1_scalar(1, BOTH, slice(384,512))
 
@@ -448,14 +447,15 @@ def tile_combnethe_pa_kernel(tc, x, W1o, b1o, W2o, b2o, W1f, b1f, W2f, b2f, out)
             if s >= 1 and s < TOTAL - 1:
                 quantise_h(s - 1, WHOLE)
                 fill()
-            follow = (s + 1, 0) if s + 1 < TOTAL else (s, 1)
             layer1_exits(s, [0])
-            layer1_passes(s, [3])
             if s + 2 < TOTAL:
                 shuffle_w1(s + 2, 1, LEFT)
             for t in range(3):
                 layer1_exits(s, [t + 1])
-                layer1_passes(follow[0], [t], [follow[1]])
+                if s + 1 < TOTAL:
+                    layer1_passes(s + 1, [t])
+            if s >= 1 and s < TOTAL - 1:
+                layer2(s - 1)
             if ROUNDS + 2 <= s < ROUNDS + 2 + T1:
                 power = sum_power(s - ROUNDS - 2, e1 if s == ROUNDS + 2 else power, rsum1)
             if s == ROUNDS + 2:
@@ -465,8 +465,10 @@ def tile_combnethe_pa_kernel(tc, x, W1o, b1o, W2o, b2o, W1f, b1f, W2f, b2f, out)
                 if s > ROUNDS + 2:
                     fill()
                 regroup_w1_scalar(s + 2, SECOND, slice(ROUTE_COLS, K_PASS))
-                regroup_w1_scalar(s + 2, FIRST, slice(V_COLS, K_PASS))
                 unload_w1(s + 2, 1, LEFT)
+                regroup_w1_scalar(s + 2, FIRST, slice(V_COLS, K_PASS))
+            if s + 1 < TOTAL:
+                layer1_passes(s + 1, [3])
             if s == ROUNDS + 1:
                 for i in range(B_TILES):
                     exponential(z1, negmax1, e1, esum1, i)
@@ -475,8 +477,6 @@ def tile_combnethe_pa_kernel(tc, x, W1o, b1o, W2o, b2o, W1f, b1f, W2f, b2f, out)
             elif (s + 2) % W2_GROUP == 0 and s + 2 < TOTAL:
                 regroup_w2((s + 2) // W2_GROUP)
                 fill()
-            if s >= 1 and s < TOTAL - 1:
-                layer2(s - 1)
             if (s + 1) % W2_GROUP == 0 and s + 1 < TOTAL:
                 quantise_w2((s + 1) // W2_GROUP)
                 fill()
@@ -496,9 +496,8 @@ def tile_combnethe_pa_kernel(tc, x, W1o, b1o, W2o, b2o, W1f, b1f, W2f, b2f, out)
         out_tiles = out.rearrange("(i p) c -> i p c", p=P)
         last = TOTAL - 1
         early, late = batch_parts(last)
-        layer1_exits(last, [0], [1])
-        layer1_passes(last, [3], [1])
-        layer1_exits(last, [1, 2, 3], [1])
+        layer1_passes(last, range(PACK), [1])
+        layer1_exits(last, range(PACK), [1])
         early_tiles, late_tiles = slice(0, B_TILES // 2), slice(B_TILES // 2, B_TILES)
         regroup_h(last, early)
         fill()

@@ -28,7 +28,7 @@ B1_ROWS = D_H // P
 B2_ROW = NETS * B1_ROWS
 RAW_BUFS = 8
 ROUTE_COLS = 256
-LAST_ROUND_PARTS = 2
+LAST_ROUND_TILES = [(0, 1), (1, 3), (3, 4)]
 V_COLS = 448
 W2_GROUP = 4
 
@@ -89,10 +89,10 @@ def tile_combnethe_pa_kernel(tc, x, W1o, b1o, W2o, b2o, W1f, b1f, W2f, b2f, out)
                     ),
                 )
 
-        def load_w1_halves(r):
+        def load_w1_halves(r, passes):
             net, g = divmod(r, ROUNDS)
             w1_raw[r] = w1_raw_pool.tile([P, IN_PASSES, PACK, K_PASS], BF16, name="w1_raw")
-            for c in range(IN_PASSES):
+            for c in passes:
                 for k in range(2):
                     half = slice(k * K_PASS // 2, (k + 1) * K_PASS // 2)
                     cols = slice(g * K_PASS + half.start, g * K_PASS + half.stop)
@@ -131,6 +131,16 @@ def tile_combnethe_pa_kernel(tc, x, W1o, b1o, W2o, b2o, W1f, b1f, W2f, b2f, out)
                 in_=route[r][:, 0 : (cols.stop - cols.start) * PACK],
             )
 
+        def quantise_w1_pass(r, c):
+            if r not in w1_codes:
+                w1_codes[r] = w1_mx_pool.tile([P, IN_PASSES, K_PASS], U32, name="w1_codes", align_bytes=64)
+                w1_scales[r] = w1_mx_pool.tile([P, IN_PASSES, K_PASS], U8, name="w1_scales", align_bytes=64)
+            nc.vector.quantize_mx(
+                out=w1_codes[r][:, c].bitcast(FP8X4),
+                scales=w1_scales[r][:, c],
+                in_=w1_grp[r][:, c].rearrange("p w j -> p (w j)"),
+            )
+
         def quantise_w1(r):
             codes = w1_mx_pool.tile([P, IN_PASSES, K_PASS], U32, name="w1_codes", align_bytes=64)
             scales = w1_mx_pool.tile([P, IN_PASSES, K_PASS], U8, name="w1_scales", align_bytes=64)
@@ -167,15 +177,16 @@ def tile_combnethe_pa_kernel(tc, x, W1o, b1o, W2o, b2o, W1f, b1f, W2f, b2f, out)
             w2_codes[q], w2_scales[q] = codes, scales
 
         def batch_parts(r):
-            n = LAST_ROUND_PARTS if r == TOTAL - 1 else 1
-            return [slice(k * B // n, (k + 1) * B // n) for k in range(n)]
+            if r < TOTAL - 1:
+                return [slice(0, B)]
+            return [slice(first * P, last * P) for first, last in LAST_ROUND_TILES]
 
         def layer1_passes(r, ts, parts=(0,)):
             for part in parts:
                 rows = batch_parts(r)[part]
                 for t in ts:
                     units = slice(t * P, (t + 1) * P)
-                    acc = psum_h.tile([P, B // len(batch_parts(r))], F32, tag="bank")
+                    acc = psum_h.tile([P, rows.stop - rows.start], F32, tag="bank")
                     for c in range(IN_PASSES):
                         nc.tensor.matmul_mx(
                             out=acc[:],
@@ -331,10 +342,14 @@ def tile_combnethe_pa_kernel(tc, x, W1o, b1o, W2o, b2o, W1f, b1f, W2f, b2f, out)
 
         x_sb = const.tile([P, B_TILES, D_IN], BF16)
         bias_rows = const.tile([P, P], BF16)
-        load_w1_halves(0)
-        for half in range(2):
-            tiles = slice(2 * half, 2 * half + 2)
-            nc.sync.dma_start(out=x_sb[:, tiles], in_=x[half * 2 * P : (half + 1) * 2 * P, :].rearrange("(i p) k -> p i k", p=P))
+        load_w1(0, [0])
+        nc.sync.dma_start(
+            out=x_sb[:, 0:2], in_=x[0:256, :].rearrange("(i p) k -> p i k", p=P)
+        )
+        nc.sync.dma_start(
+            out=x_sb[:, 2:4], in_=x[256:512, :].rearrange("(i p) k -> p i k", p=P)
+        )
+        load_w1(0, [1])
         nc.gpsimd.memset(bias_rows[:], 0.0)
         for net in range(NETS):
             nc.sync.dma_start(
@@ -376,7 +391,7 @@ def tile_combnethe_pa_kernel(tc, x, W1o, b1o, W2o, b2o, W1f, b1f, W2f, b2f, out)
         x_codes = const.tile([P, IN_PASSES, B], U32, align_bytes=64)
         x_scales = const.tile([P, IN_PASSES, B], U8, align_bytes=64)
 
-        def transpose_x(half):
+        def transpose_x(half, copies):
             for c in range(IN_PASSES):
                 xt = psum_h.tile([P, 2, 2 * P], F32, tag="bank")
                 for u in range(2):
@@ -384,7 +399,7 @@ def tile_combnethe_pa_kernel(tc, x, W1o, b1o, W2o, b2o, W1f, b1f, W2f, b2f, out)
                         nc.tensor.transpose(
                             out=xt[:, u, ii * P : (ii + 1) * P], in_=x_words[:, 2 * half + ii, c, u, :], identity=ident[:]
                         )
-                nc.scalar.copy(
+                copies[c](
                     out=x_grp_words[:, c, half * 2 * P : (half + 1) * 2 * P, :],
                     in_=xt[:].rearrange("p u b -> p b u"),
                 )
@@ -399,20 +414,22 @@ def tile_combnethe_pa_kernel(tc, x, W1o, b1o, W2o, b2o, W1f, b1f, W2f, b2f, out)
         FIRST, SECOND, BOTH = slice(0, 1), slice(1, 2), slice(0, 2)
         L, R = slice(0, 256), slice(256, 512)
         FIRST, SECOND, BOTH = slice(0, 1), slice(1, 2), slice(0, 2)
-        regroup_w1_vector(0, FIRST, L)
-        regroup_w1_scalar(0, FIRST, R)
-        regroup_w1_vector(0, SECOND, L)
-        regroup_w1_vector(0, SECOND, slice(256, 384))
-        regroup_w1_scalar(0, SECOND, slice(384, 512))
-        quantise_w1(0)
-        transpose_x(0)
-        transpose_x(1)
+        regroup_w1_vector(0, FIRST, slice(0, 256))
+        regroup_w1_scalar(0, FIRST, slice(256, 512))
+        quantise_w1_pass(0, 0)
+        transpose_x(0, (nc.scalar.copy, nc.scalar.copy))
+        transpose_x(1, (nc.scalar.copy, nc.scalar.copy))
+        regroup_w1_vector(0, SECOND, slice(0, 512))
+        quantise_x()
+        quantise_w1_pass(0, 1)
         bias_rows_f32 = const.tile([P, P], F32)
         nc.scalar.copy(out=bias_rows_f32[:], in_=bias_rows[:])
         bias_ps = psum_l.tile([P, P], F32, name="logits0")
         nc.tensor.transpose(out=bias_ps[:], in_=bias_rows_f32[:], identity=ident[:])
+        regroup_w1_scalar(1, FIRST, slice(256, 512))
         bias_cols = const.tile([P, P], F32)
         nc.scalar.copy(out=bias_cols[:], in_=bias_ps[:])
+        layer1_passes(0, range(PACK))
         b2_ps = psum_l.tile([P, NETS, C], F32, name="logits1")
         for net in range(NETS):
             nc.tensor.matmul(
@@ -422,14 +439,9 @@ def tile_combnethe_pa_kernel(tc, x, W1o, b1o, W2o, b2o, W1f, b1f, W2f, b2f, out)
                 start=True,
                 stop=True,
             )
-        regroup_w1_vector(1, FIRST, slice(0,384))
-        quantise_x()
-        layer1_passes(0, range(PACK))
-        regroup_w1_vector(1, SECOND, slice(0,384))
-        regroup_w1_scalar(1, BOTH, slice(384,512))
-
-        b2_bc = const.tile([P, NETS, C], F32)
-        nc.scalar.copy(out=b2_bc[:], in_=b2_ps[:])
+        regroup_w1_vector(1, FIRST, slice(0, 256))
+        regroup_w1_vector(1, SECOND, slice(0, 256))
+        regroup_w1_scalar(1, SECOND, slice(256, 512))
         LEFT = slice(0, ROUTE_COLS)
         WHOLE = slice(0, B)
         for s in range(TOTAL):
@@ -454,6 +466,9 @@ def tile_combnethe_pa_kernel(tc, x, W1o, b1o, W2o, b2o, W1f, b1f, W2f, b2f, out)
                 layer1_exits(s, [t + 1])
                 if s + 1 < TOTAL:
                     layer1_passes(s + 1, [t])
+            if s == 0:
+                b2_bc = const.tile([P, NETS, C], F32)
+                nc.scalar.copy(out=b2_bc[:], in_=b2_ps[:])
             if s >= 1 and s < TOTAL - 1:
                 layer2(s - 1)
             if ROUNDS + 2 <= s < ROUNDS + 2 + T1:
@@ -495,36 +510,49 @@ def tile_combnethe_pa_kernel(tc, x, W1o, b1o, W2o, b2o, W1f, b1f, W2f, b2f, out)
         result = soft.tile([P, B_TILES, C], F32)
         out_tiles = out.rearrange("(i p) c -> i p c", p=P)
         last = TOTAL - 1
-        early, late = batch_parts(last)
-        layer1_passes(last, range(PACK), [1])
-        layer1_exits(last, range(PACK), [1])
-        early_tiles, late_tiles = slice(0, B_TILES // 2), slice(B_TILES // 2, B_TILES)
-        regroup_h(last, early)
+        parts = batch_parts(last)
+        tiles = [slice(*pair) for pair in LAST_ROUND_TILES]
+        for k in range(1, len(parts)):
+            layer1_passes(last, range(PACK), [k])
+            layer1_exits(last, range(PACK), [k])
+        regroup_h(last, parts[0])
         fill()
         quantise_h(last - 1, WHOLE)
         fill()
         layer2(last - 1)
-        quantise_h(last, early)
-        fill()
-        layer2(last, range(0, B_TILES // 2))
-        regroup_h(last, late)
-        fill(len(gate_queue))
-        share1 = soft.tile([P, B_TILES, C], F32)
-        for i in range(B_TILES):
-            nc.scalar.activation(out=share1[:, i, :], in_=e1[:, i, :], func=ACT.Copy, scale=keep[:, i : i + 1])
-        quantise_h(last, late)
-        for i in range(0, B_TILES // 2):
+        for k in range(len(parts)):
+            if k + 1 < len(parts):
+                quantise_h(last, parts[k])
+                if k == 0:
+                    fill()
+                layer2(last, range(tiles[k].start, tiles[k].stop))
+                regroup_h(last, parts[k + 1])
+            else:
+                quantise_h(last, parts[k])
+                layer2(last, range(tiles[k].start, tiles[k].stop))
+            if k == 0:
+                fill(len(gate_queue))
+                share1 = soft.tile([P, B_TILES, C], F32)
+                for i in range(B_TILES):
+                    nc.scalar.activation(
+                        out=share1[:, i, :], in_=e1[:, i, :], func=ACT.Copy, scale=keep[:, i : i + 1]
+                    )
+            else:
+                for i in range(tiles[k - 1].start, tiles[k - 1].stop):
+                    add_b2(1, z2, i)
+                if k > 1:
+                    row_max(z2, negmax2, tiles[k - 2])
+                    for i in range(tiles[k - 2].start, tiles[k - 2].stop):
+                        exponential(z2, negmax2, e2, esum2, i)
+        row_max(z2, negmax2, tiles[-2])
+        for i in range(tiles[-1].start, tiles[-1].stop):
             add_b2(1, z2, i)
-        layer2(last, range(B_TILES // 2, B_TILES))
-        row_max(z2, negmax2, early_tiles)
-        for i in range(B_TILES // 2, B_TILES):
-            add_b2(1, z2, i)
-        for i in range(0, B_TILES // 2):
+        for i in range(tiles[-2].start, tiles[-2].stop):
             exponential(z2, negmax2, e2, esum2, i)
-        row_max(z2, negmax2, late_tiles)
-        for i in range(B_TILES // 2, B_TILES):
+        row_max(z2, negmax2, tiles[-1])
+        for i in range(tiles[-1].start, tiles[-1].stop):
             exponential(z2, negmax2, e2, esum2, i)
-        for pair in (early_tiles, late_tiles):
+        for pair in tiles:
             nc.vector.reciprocal(out=weight2[:, pair], in_=esum2[:, pair])
             for i in range(pair.start, pair.stop):
                 nc.vector.tensor_scalar_mul(out=z2[:, i, :], in0=e2[:, i, :], scalar1=cond[:, i : i + 1])

@@ -380,6 +380,14 @@ def tile_combnethe_pa_kernel(tc, x, W1o, b1o, W2o, b2o, W1f, b1f, W2f, b2f, out)
         nc.vector.memset(warm[:], 0.0)
         nc.scalar.activation(out=warm[:], in_=warm[:], func=ACT.Exp)
 
+        zeros = const.tile([P, K_PASS], BF16)
+        nc.vector.memset(zeros[:], 0.0)
+        busy_bank = psum_l.tile([P, K_PASS], F32, name="logits3")
+
+        def keep_busy(count):
+            for k in range(count):
+                nc.tensor.matmul(out=busy_bank[:], lhsT=zeros[:, 0:P], rhs=zeros[:], start=True, stop=True)
+
         ident = const.tile([P, P], F32)
         make_identity(nc, ident[:])
         ident_bf = const.tile([P, P], BF16)
@@ -417,6 +425,7 @@ def tile_combnethe_pa_kernel(tc, x, W1o, b1o, W2o, b2o, W1f, b1f, W2f, b2f, out)
         regroup_w1_vector(0, FIRST, slice(0, 256))
         regroup_w1_scalar(0, FIRST, slice(256, 512))
         quantise_w1_pass(0, 0)
+        keep_busy(6)
         transpose_x(0, (nc.scalar.copy, nc.scalar.copy))
         transpose_x(1, (nc.scalar.copy, nc.scalar.copy))
         regroup_w1_vector(0, SECOND, slice(0, 512))
@@ -425,7 +434,9 @@ def tile_combnethe_pa_kernel(tc, x, W1o, b1o, W2o, b2o, W1f, b1f, W2f, b2f, out)
         bias_rows_f32 = const.tile([P, P], F32)
         nc.scalar.copy(out=bias_rows_f32[:], in_=bias_rows[:])
         bias_ps = psum_l.tile([P, P], F32, name="logits0")
+        keep_busy(4)
         nc.tensor.transpose(out=bias_ps[:], in_=bias_rows_f32[:], identity=ident[:])
+        keep_busy(3)
         regroup_w1_scalar(1, FIRST, slice(256, 512))
         bias_cols = const.tile([P, P], F32)
         nc.scalar.copy(out=bias_cols[:], in_=bias_ps[:])

@@ -344,10 +344,10 @@ def tile_combnethe_pa_kernel(tc, x, W1o, b1o, W2o, b2o, W1f, b1f, W2f, b2f, out)
         bias_rows = const.tile([P, P], BF16)
         load_w1(0, [0])
         nc.sync.dma_start(
-            out=x_sb[:, 0:2], in_=x[0:256, :].rearrange("(i p) k -> p i k", p=P)
+            out=x_sb[:, 0:2], in_=x.rearrange("(p i) k -> p i k", i=B_TILES)[:, 0:2]
         )
         nc.sync.dma_start(
-            out=x_sb[:, 2:4], in_=x[256:512, :].rearrange("(i p) k -> p i k", p=P)
+            out=x_sb[:, 2:4], in_=x.rearrange("(p i) k -> p i k", i=B_TILES)[:, 2:4]
         )
         load_w1(0, [1])
         nc.gpsimd.memset(bias_rows[:], 0.0)
@@ -460,6 +460,8 @@ def tile_combnethe_pa_kernel(tc, x, W1o, b1o, W2o, b2o, W1f, b1f, W2f, b2f, out)
                 z1, negmax1, e1, esum1 = softmax_tiles(0)
                 for i in range(B_TILES):
                     add_b2(0, z1, i)
+            if s == 0:
+                regroup_w1_vector(2, FIRST, slice(0, V_COLS))
             if s + 1 < TOTAL:
                 quantise_w1(s + 1)
                 fill()
@@ -487,7 +489,8 @@ def tile_combnethe_pa_kernel(tc, x, W1o, b1o, W2o, b2o, W1f, b1f, W2f, b2f, out)
             if s == ROUNDS + 2:
                 gate_queue.extend(gate_stages())
             if s + 2 < TOTAL:
-                regroup_w1_vector(s + 2, FIRST, slice(0, V_COLS))
+                if s > 0:
+                    regroup_w1_vector(s + 2, FIRST, slice(0, V_COLS))
                 if s > ROUNDS + 2:
                     fill()
                 regroup_w1_scalar(s + 2, SECOND, slice(ROUTE_COLS, K_PASS))
@@ -507,8 +510,13 @@ def tile_combnethe_pa_kernel(tc, x, W1o, b1o, W2o, b2o, W1f, b1f, W2f, b2f, out)
                 quantise_w2((s + 1) // W2_GROUP)
                 fill()
             if s < TOTAL - 1:
-                regroup_h(s, WHOLE)
-                fill(1 if s < ROUNDS + 3 else 2)
+                if s < ROUNDS + 3:
+                    regroup_h(s, WHOLE)
+                    fill()
+                else:
+                    for half in range(2):
+                        regroup_h(s, slice(half * B // 2, (half + 1) * B // 2))
+                        fill()
             if s == 0:
                 quantise_w2(0)
             if (s + 2) % W2_GROUP == 0 and s + 2 + W2_GROUP < TOTAL:
@@ -519,7 +527,7 @@ def tile_combnethe_pa_kernel(tc, x, W1o, b1o, W2o, b2o, W1f, b1f, W2f, b2f, out)
         z2, negmax2, e2, esum2 = softmax_tiles(1)
         weight2 = small.tile([P, B_TILES], F32)
         result = soft.tile([P, B_TILES, C], F32)
-        out_tiles = out.rearrange("(i p) c -> i p c", p=P)
+        out_tiles = out.rearrange("(p i) c -> i p c", i=B_TILES)
         last = TOTAL - 1
         parts = batch_parts(last)
         tiles = [slice(*pair) for pair in LAST_ROUND_TILES]

@@ -117,9 +117,9 @@ def tile_combnethe_pa_kernel(tc, x, W1o, b1o, W2o, b2o, W1f, b1f, W2f, b2f, out)
             for first in range(cols.start, cols.stop, P):
                 to = (first - cols.start) * PACK
                 nc.tensor.matmul(
-                    out=bank[:, to : to + P * PACK],
+                    out=bank[:, to : to + P * PACK].rearrange("p (w j) -> p j w", j=PACK),
                     lhsT=ident_bf[:],
-                    rhs=w1_raw[r][:, c, :, first : first + P].rearrange("p j w -> p w j"),
+                    rhs=w1_raw[r][:, c, :, first : first + P],
                     start=True,
                     stop=True,
                 )

from contextlib import ExitStack
from functools import partial

import concourse.mybir as mybir
from concourse.masks import make_identity

F32 = mybir.dt.float32
BF16 = mybir.dt.bfloat16
U32 = mybir.dt.uint32
U8 = mybir.dt.uint8
FP8X4 = mybir.dt.float8_e4m3fn_x4
ACT = mybir.ActivationFunctionType
ALU = mybir.AluOpType
AX = mybir.AxisListType

P = 128
PACK = 4
K_PASS = P * PACK

B, D_IN, D_H, C = 512, 1024, 4096, 128
TAU, T1, T2 = 0.5, 3, 3
NETS = 2
IN_PASSES = D_IN // K_PASS
ROUNDS = D_H // K_PASS
TOTAL = NETS * ROUNDS
B_TILES = B // P
B1_ROWS = D_H // P
B2_ROW = NETS * B1_ROWS
RAW_BUFS = 8
ROUTE_COLS = 256
LAST_ROUND_TILES = [(0, 1), (1, 3), (3, 4)]
V_COLS = 448
W2_GROUP = 4

FLOPS = NETS * (2 * B * D_IN * D_H + 2 * B * D_H * C)


def regroup(copy, grouped, planes):
    copy(
        out=grouped.rearrange("p (c i) j -> p c j i", i=4),
        in_=planes.rearrange("p j (c i) -> p c j i", i=4),
    )


def regroup2(copy, grouped, planes):
    copy(
        out=grouped.rearrange("p a (c i) j -> p a c j i", i=4),
        in_=planes.rearrange("p a j (c i) -> p a c j i", i=4),
    )


def tile_combnethe_pa_kernel(tc, x, W1o, b1o, W2o, b2o, W1f, b1f, W2f, b2f, out):
    nc = tc.nc
    W1, b1, W2, b2 = (W1o, W1f), (b1o, b1f), (W2o, W2f), (b2o, b2f)
    with ExitStack() as ctx:
        ctx.enter_context(
            tc.manual_schedule(
                engines={mybir.EngineType.DVE, mybir.EngineType.Activation, mybir.EngineType.PE}
            )
        )
        const = ctx.enter_context(tc.tile_pool(name="const", bufs=1))
        w1_raw_pool = ctx.enter_context(tc.tile_pool(name="w1_raw", bufs=RAW_BUFS))
        w1_grp_pool = ctx.enter_context(tc.tile_pool(name="w1_grp", bufs=3))
        w1_mx_pool = ctx.enter_context(tc.tile_pool(name="w1_mx", bufs=3))
        w2_pool = ctx.enter_context(tc.tile_pool(name="w2", bufs=2))
        h_pool = ctx.enter_context(tc.tile_pool(name="h", bufs=3))
        soft = ctx.enter_context(tc.tile_pool(name="soft", bufs=1))
        small = ctx.enter_context(tc.tile_pool(name="small", bufs=1))
        psum_h = ctx.enter_context(tc.psum_pool(name="psum_h", bufs=4))
        psum_l = ctx.enter_context(tc.psum_pool(name="psum_l", bufs=1))

        w1_raw, w1_grp, w1_codes, w1_scales = {}, {}, {}, {}
        w2_raw, w2_grp, w2_codes, w2_scales = {}, {}, {}, {}
        h_banks, h_planes, h_grp, h_codes, h_scales = {}, {}, {}, {}, {}
        logits = {}
        gate_queue = []
        route = {}

        def load_w1(r, passes=range(IN_PASSES)):
            net, g = divmod(r, ROUNDS)
            if r not in w1_raw:
                w1_raw[r] = w1_raw_pool.tile([P, IN_PASSES, PACK, K_PASS], BF16, name="w1_raw")
            raw = w1_raw[r]
            for c in passes:
                nc.sync.dma_start(
                    out=raw[:, c],
                    in_=W1[net][c * K_PASS : (c + 1) * K_PASS, g * K_PASS : (g + 1) * K_PASS].rearrange(
                        "(p j) w -> p j w", j=PACK
                    ),
                )

        def load_w1_halves(r, passes):
            net, g = divmod(r, ROUNDS)
            w1_raw[r] = w1_raw_pool.tile([P, IN_PASSES, PACK, K_PASS], BF16, name="w1_raw")
            for c in passes:
                for k in range(2):
                    half = slice(k * K_PASS // 2, (k + 1) * K_PASS // 2)
                    cols = slice(g * K_PASS + half.start, g * K_PASS + half.stop)
                    nc.sync.dma_start(
                        out=w1_raw[r][:, c, :, half],
                        in_=W1[net][c * K_PASS : (c + 1) * K_PASS, cols].rearrange("(p j) w -> p j w", j=PACK),
                    )

        def w1_grouped(r):
            if r not in w1_grp:
                w1_grp[r] = w1_grp_pool.tile([P, IN_PASSES, K_PASS, PACK], BF16, name="w1_grp", align_bytes=64)
            return w1_grp[r]

        def regroup_w1_vector(r, passes, cols=slice(0, V_COLS)):
            regroup2(nc.vector.tensor_copy, w1_grouped(r)[:, passes, cols], w1_raw[r][:, passes, :, cols])

        def regroup_w1_scalar(r, passes, cols=slice(V_COLS, K_PASS)):
            regroup2(nc.scalar.copy, w1_grouped(r)[:, passes, cols], w1_raw[r][:, passes, :, cols])

        def shuffle_w1(r, c, cols):
            bank = psum_h.tile([P, ROUTE_COLS * PACK], BF16, tag="bank")
            for first in range(cols.start, cols.stop, P):
                to = (first - cols.start) * PACK
                nc.tensor.matmul(
                    out=bank[:, to : to + P * PACK].rearrange("p (w j) -> p j w", j=PACK),
                    lhsT=ident_bf[:],
                    rhs=w1_raw[r][:, c, :, first : first + P],
                    start=True,
                    stop=True,
                )
            route[r] = bank

        def unload_w1(r, c, cols):
            nc.scalar.copy(
                out=w1_grouped(r)[:, c, cols].rearrange("p w j -> p (w j)"),
                in_=route[r][:, 0 : (cols.stop - cols.start) * PACK],
            )

        def quantise_w1_pass(r, c):
            if r not in w1_codes:
                w1_codes[r] = w1_mx_pool.tile([P, IN_PASSES, K_PASS], U32, name="w1_codes", align_bytes=64)
                w1_scales[r] = w1_mx_pool.tile([P, IN_PASSES, K_PASS], U8, name="w1_scales", align_bytes=64)
            nc.vector.quantize_mx(
                out=w1_codes[r][:, c].bitcast(FP8X4),
                scales=w1_scales[r][:, c],
                in_=w1_grp[r][:, c].rearrange("p w j -> p (w j)"),
            )

        def quantise_w1(r):
            codes = w1_mx_pool.tile([P, IN_PASSES, K_PASS], U32, name="w1_codes", align_bytes=64)
            scales = w1_mx_pool.tile([P, IN_PASSES, K_PASS], U8, name="w1_scales", align_bytes=64)
            nc.vector.quantize_mx(
                out=codes[:].rearrange("p c w -> p (c w)").bitcast(FP8X4),
                scales=scales[:].rearrange("p c w -> p (c w)"),
                in_=w1_grp[r][:].rearrange("p c w j -> p (c w j)"),
            )
            w1_codes[r], w1_scales[r] = codes, scales

        def load_w2(q):
            net, g = divmod(q * W2_GROUP, ROUNDS)
            raw = w2_pool.tile([P, PACK, W2_GROUP * C], BF16, name="w2_raw")
            for k in range(W2_GROUP):
                rows = slice((g + k) * K_PASS, (g + k + 1) * K_PASS)
                nc.sync.dma_start(
                    out=raw[:, :, k * C : (k + 1) * C], in_=W2[net][rows, :].rearrange("(t p) n -> p t n", p=P)
                )
            w2_raw[q] = raw

        def regroup_w2(q):
            grp = w2_pool.tile([P, W2_GROUP * C, PACK], BF16, name="w2_grp", align_bytes=64)
            regroup(nc.vector.tensor_copy, grp[:], w2_raw[q][:])
            w2_grp[q] = grp

        def quantise_w2(q):
            codes = w2_pool.tile([P, W2_GROUP, C], U32, name="w2_codes", align_bytes=64)
            scales = w2_pool.tile([P, W2_GROUP, C], U8, name="w2_scales", align_bytes=64)
            nc.vector.quantize_mx(
                out=codes[:].rearrange("p g n -> p (g n)").bitcast(FP8X4),
                scales=scales[:].rearrange("p g n -> p (g n)"),
                in_=w2_grp[q][:].rearrange("p w t -> p (w t)"),
            )
            w2_codes[q], w2_scales[q] = codes, scales

        def batch_parts(r):
            if r < TOTAL - 1:
                return [slice(0, B)]
            return [slice(first * P, last * P) for first, last in LAST_ROUND_TILES]

        def layer1_passes(r, ts, parts=(0,)):
            for part in parts:
                rows = batch_parts(r)[part]
                for t in ts:
                    units = slice(t * P, (t + 1) * P)
                    acc = psum_h.tile([P, rows.stop - rows.start], F32, tag="bank")
                    for c in range(IN_PASSES):
                        nc.tensor.matmul_mx(
                            out=acc[:],
                            lhsT=w1_codes[r][:, c, units].bitcast(FP8X4),
                            lhsT_scale=w1_scales[r][:, c, units],
                            rhs=x_codes[:, c, rows].bitcast(FP8X4),
                            rhs_scale=x_scales[:, c, rows],
                            start=(c == 0),
                            stop=(c == IN_PASSES - 1),
                        )
                    h_banks[r, part, t] = acc

        def layer1_exits(r, ts, parts=(0,)):
            if r not in h_planes:
                h_planes[r] = h_pool.tile([P, PACK, B], BF16, name="h_planes")
            for part in parts:
                for t in ts:
                    col = r * PACK + t
                    nc.scalar.activation(
                        out=h_planes[r][:, t, batch_parts(r)[part]],
                        in_=h_banks[r, part, t][:],
                        func=ACT.Relu,
                        bias=bias_cols[:, col : col + 1],
                        scale=1.0,
                    )

        def h_grouped(r):
            if r not in h_grp:
                h_grp[r] = h_pool.tile([P, B, PACK], BF16, name="h_grp", align_bytes=64)
                h_codes[r] = h_pool.tile([P, B], U32, name="h_codes", align_bytes=64)
                h_scales[r] = h_pool.tile([P, B], U8, name="h_scales", align_bytes=64)
            return h_grp[r]

        def regroup_h(r, rows):
            regroup(nc.vector.tensor_copy, h_grouped(r)[:, rows, :], h_planes[r][:, :, rows])

        def quantise_h(r, rows):
            nc.vector.quantize_mx(
                out=h_codes[r][:, rows].bitcast(FP8X4),
                scales=h_scales[r][:, rows],
                in_=h_grp[r][:, rows, :].rearrange("p b t -> p (b t)"),
            )

        def layer2(r, tiles=range(B_TILES)):
            net, g = divmod(r, ROUNDS)
            for i in tiles:
                if g == 0:
                    bank = psum_l.tile([P, C], F32, name="logits%d" % i)
                    logits[i] = bank
                rows = slice(i * P, (i + 1) * P)
                nc.tensor.matmul_mx(
                    out=logits[i][:],
                    lhsT=h_codes[r][:, rows].bitcast(FP8X4),
                    lhsT_scale=h_scales[r][:, rows],
                    rhs=w2_codes[r // W2_GROUP][:, r % W2_GROUP].bitcast(FP8X4),
                    rhs_scale=w2_scales[r // W2_GROUP][:, r % W2_GROUP],
                    start=(g == 0),
                    stop=(g == ROUNDS - 1),
                )

        def softmax_tiles(net):
            z = soft.tile([P, B_TILES, C], F32, name="z%d" % net)
            negmax = small.tile([P, B_TILES], F32, name="negmax%d" % net)
            e = soft.tile([P, B_TILES, C], F32, name="e%d" % net)
            esum = small.tile([P, B_TILES], F32, name="esum%d" % net)
            return z, negmax, e, esum

        def add_b2(net, z, i):
            nc.vector.tensor_tensor(out=z[:, i, :], in0=logits[i][:], in1=b2_bc[:, net, :], op=ALU.add)

        def row_max(z, negmax, tiles):
            nc.vector.tensor_reduce(out=negmax[:, tiles], in_=z[:, tiles, :], axis=AX.X, op=ALU.max, negate=True)

        def exponential(z, negmax, e, esum, i):
            nc.scalar.activation(
                out=e[:, i, :],
                in_=z[:, i, :],
                func=ACT.Exp,
                bias=negmax[:, i : i + 1],
                scale=1.0,
                accum_out=esum[:, i : i + 1],
            )

        def sum_power(k, e, rsum):
            squared = soft.tile([P, B_TILES, C], F32, name="power%d" % k)
            for i in range(B_TILES):
                nc.scalar.activation(
                    out=squared[:, i, :],
                    in_=e[:, i, :],
                    func=ACT.Square,
                    scale=(rsum[:, i : i + 1] if k == 0 else 1.0),
                    accum_out=power_sums[:, k, i : i + 1],
                )
            return squared

        def gate_stages():
            v = nc.vector
            stages = []

            def stage(*calls):
                stages.append(calls)

            for k in range(T1):
                m = 2.0 + TAU * TAU if k == 0 else 2.0
                u, r = gate_u[:, k], gate_r[:, k]
                shift = partial(v.tensor_scalar_add, out=u, in0=power_sums[:, k], scalar1=TAU ** (2 ** (k + 1)))
                if k == 0:
                    stage(shift)
                    row_sum = u
                else:
                    stage(shift, partial(v.tensor_mul, out=gate_t[:], in0=gate_f[:], in1=gate_f[:]))
                    stage(partial(v.tensor_mul, out=gate_t[:], in0=gate_t[:], in1=u))
                    row_sum = gate_t[:]
                stage(
                    partial(
                        v.tensor_scalar,
                        out=gate_b[:],
                        in0=row_sum,
                        scalar1=-2.0 / m,
                        scalar2=1.0,
                        op0=ALU.mult,
                        op1=ALU.add,
                    ),
                    partial(v.reciprocal, out=r, in_=u),
                )
                for step in range(T2 + 1):
                    stage(partial(v.tensor_mul, out=gate_b[:], in0=gate_b[:], in1=gate_b[:]))
                stage(
                    partial(
                        v.scalar_tensor_tensor,
                        out=gate_f[:],
                        in0=gate_b[:],
                        scalar=1.0,
                        in1=r,
                        op0=ALU.subtract,
                        op1=ALU.mult,
                    )
                )
            tau_end = TAU ** (2**T1)
            stage(
                partial(v.tensor_scalar_mul, out=cond[:], in0=gate_f[:], scalar1=-tau_end),
                partial(
                    v.tensor_scalar, out=keep[:], in0=gate_f[:], scalar1=tau_end, scalar2=1.0, op0=ALU.mult, op1=ALU.add
                ),
            )
            stage(partial(v.tensor_mul, out=keep[:], in0=keep[:], in1=rsum1[:]))
            return stages

        def fill(count=1):
            for step in range(min(count, len(gate_queue))):
                for call in gate_queue.pop(0):
                    call()

        x_sb = const.tile([P, B_TILES, D_IN], BF16)
        bias_rows = const.tile([P, P], BF16)
        load_w1(0, [0])
        nc.sync.dma_start(
            out=x_sb[:, 0:2], in_=x.rearrange("(p i) k -> p i k", i=B_TILES)[:, 0:2]
        )
        nc.sync.dma_start(
            out=x_sb[:, 2:4], in_=x.rearrange("(p i) k -> p i k", i=B_TILES)[:, 2:4]
        )
        load_w1(0, [1])
        nc.gpsimd.memset(bias_rows[:], 0.0)
        for net in range(NETS):
            nc.sync.dma_start(
                out=bias_rows[net * B1_ROWS : (net + 1) * B1_ROWS, :], in_=b1[net].rearrange("(r p) -> r p", p=P)
            )
            nc.sync.dma_start(
                out=bias_rows[B2_ROW + net : B2_ROW + net + 1, :], in_=b2[net].rearrange("(o c) -> o c", o=1)
            )
        load_w1(1)
        load_w1(2)
        load_w2(0)
        load_w1(3)
        load_w2(1)
        for r in range(4, RAW_BUFS):
            load_w1(r)

        power_sums = small.tile([P, T1, B_TILES], F32)
        gate_u = small.tile([P, T1, B_TILES], F32)
        gate_r = small.tile([P, T1, B_TILES], F32)
        gate_t = small.tile([P, B_TILES], F32)
        gate_b = small.tile([P, B_TILES], F32)
        gate_f = small.tile([P, B_TILES], F32)
        cond = small.tile([P, B_TILES], F32)
        keep = small.tile([P, B_TILES], F32)
        rsum1 = small.tile([P, B_TILES], F32)

        warm = const.tile([P, 1], F32)
        nc.vector.memset(warm[:], 0.0)
        nc.scalar.activation(out=warm[:], in_=warm[:], func=ACT.Exp)

        zeros = const.tile([P, K_PASS], BF16)
        nc.vector.memset(zeros[:], 0.0)
        busy_bank = psum_l.tile([P, K_PASS], F32, name="logits3")

        def keep_busy(count):
            for k in range(count):
                nc.tensor.matmul(out=busy_bank[:], lhsT=zeros[:, 0:P], rhs=zeros[:], start=True, stop=True)

        ident = const.tile([P, P], F32)
        make_identity(nc, ident[:])
        ident_bf = const.tile([P, P], BF16)
        make_identity(nc, ident_bf[:])

        x_words = x_sb[:].bitcast(F32).rearrange("p i (c q u) -> p i c u q", c=IN_PASSES, u=2)
        x_grp = const.tile([P, IN_PASSES, B, PACK], BF16, align_bytes=64)
        x_grp_words = x_grp[:].bitcast(F32)
        x_codes = const.tile([P, IN_PASSES, B], U32, align_bytes=64)
        x_scales = const.tile([P, IN_PASSES, B], U8, align_bytes=64)

        def transpose_x(half, copies):
            for c in range(IN_PASSES):
                xt = psum_h.tile([P, 2, 2 * P], F32, tag="bank")
                for u in range(2):
                    for ii in range(2):
                        nc.tensor.transpose(
                            out=xt[:, u, ii * P : (ii + 1) * P], in_=x_words[:, 2 * half + ii, c, u, :], identity=ident[:]
                        )
                copies[c](
                    out=x_grp_words[:, c, half * 2 * P : (half + 1) * 2 * P, :],
                    in_=xt[:].rearrange("p u b -> p b u"),
                )

        def quantise_x():
            nc.vector.quantize_mx(
                out=x_codes[:].rearrange("p c b -> p (c b)").bitcast(FP8X4),
                scales=x_scales[:].rearrange("p c b -> p (c b)"),
                in_=x_grp[:].rearrange("p c b t -> p (c b t)"),
            )

        FIRST, SECOND, BOTH = slice(0, 1), slice(1, 2), slice(0, 2)
        L, R = slice(0, 256), slice(256, 512)
        FIRST, SECOND, BOTH = slice(0, 1), slice(1, 2), slice(0, 2)
        regroup_w1_vector(0, FIRST, slice(0, 256))
        regroup_w1_scalar(0, FIRST, slice(256, 512))
        quantise_w1_pass(0, 0)
        keep_busy(6)
        transpose_x(0, (nc.scalar.copy, nc.scalar.copy))
        transpose_x(1, (nc.scalar.copy, nc.scalar.copy))
        regroup_w1_vector(0, SECOND, slice(0, 512))
        quantise_x()
        quantise_w1_pass(0, 1)
        bias_rows_f32 = const.tile([P, P], F32)
        nc.scalar.copy(out=bias_rows_f32[:], in_=bias_rows[:])
        bias_ps = psum_l.tile([P, P], F32, name="logits0")
        keep_busy(4)
        nc.tensor.transpose(out=bias_ps[:], in_=bias_rows_f32[:], identity=ident[:])
        keep_busy(3)
        regroup_w1_scalar(1, FIRST, slice(256, 512))
        bias_cols = const.tile([P, P], F32)
        nc.scalar.copy(out=bias_cols[:], in_=bias_ps[:])
        layer1_passes(0, range(PACK))
        b2_ps = psum_l.tile([P, NETS, C], F32, name="logits1")
        for net in range(NETS):
            nc.tensor.matmul(
                out=b2_ps[:, net, :],
                lhsT=bias_cols[:, B2_ROW + net : B2_ROW + net + 1].to_broadcast([P, P]),
                rhs=ident[:],
                start=True,
                stop=True,
            )
        regroup_w1_vector(1, FIRST, slice(0, 256))
        regroup_w1_vector(1, SECOND, slice(0, 256))
        regroup_w1_scalar(1, SECOND, slice(256, 512))
        LEFT = slice(0, ROUTE_COLS)
        WHOLE = slice(0, B)
        for s in range(TOTAL):
            if s == ROUNDS + 1:
                z1, negmax1, e1, esum1 = softmax_tiles(0)
                for i in range(B_TILES):
                    add_b2(0, z1, i)
            if s == 0:
                regroup_w1_vector(2, FIRST, slice(0, V_COLS))
            if s + 1 < TOTAL:
                quantise_w1(s + 1)
                fill()
            if s == ROUNDS + 2:
                nc.vector.reciprocal(out=rsum1[:], in_=esum1[:])
            if s == ROUNDS + 1:
                row_max(z1, negmax1, slice(0, B_TILES))
            if s >= 1 and s < TOTAL - 1:
                quantise_h(s - 1, WHOLE)
                fill()
            layer1_exits(s, [0])
            if s + 2 < TOTAL:
                shuffle_w1(s + 2, 1, LEFT)
            for t in range(3):
                layer1_exits(s, [t + 1])
                if s + 1 < TOTAL:
                    layer1_passes(s + 1, [t])
            if s == 0:
                b2_bc = const.tile([P, NETS, C], F32)
                nc.scalar.copy(out=b2_bc[:], in_=b2_ps[:])
            if s >= 1 and s < TOTAL - 1:
                layer2(s - 1)
            if ROUNDS + 2 <= s < ROUNDS + 2 + T1:
                power = sum_power(s - ROUNDS - 2, e1 if s == ROUNDS + 2 else power, rsum1)
            if s == ROUNDS + 2:
                gate_queue.extend(gate_stages())
            if s + 2 < TOTAL:
                if s > 0:
                    regroup_w1_vector(s + 2, FIRST, slice(0, V_COLS))
                if s > ROUNDS + 2:
                    fill()
                regroup_w1_scalar(s + 2, SECOND, slice(ROUTE_COLS, K_PASS))
                unload_w1(s + 2, 1, LEFT)
                regroup_w1_scalar(s + 2, FIRST, slice(V_COLS, K_PASS))
            if s + 1 < TOTAL:
                layer1_passes(s + 1, [3])
            if s == ROUNDS + 1:
                for i in range(B_TILES):
                    exponential(z1, negmax1, e1, esum1, i)
            if s == 0:
                regroup_w2(0)
            elif (s + 2) % W2_GROUP == 0 and s + 2 < TOTAL:
                regroup_w2((s + 2) // W2_GROUP)
                fill()
            if (s + 1) % W2_GROUP == 0 and s + 1 < TOTAL:
                quantise_w2((s + 1) // W2_GROUP)
                fill()
            if s < TOTAL - 1:
                if s < ROUNDS + 3:
                    regroup_h(s, WHOLE)
                    fill()
                else:
                    for half in range(2):
                        regroup_h(s, slice(half * B // 2, (half + 1) * B // 2))
                        fill()
            if s == 0:
                quantise_w2(0)
            if (s + 2) % W2_GROUP == 0 and s + 2 + W2_GROUP < TOTAL:
                load_w2((s + 2) // W2_GROUP + 1)
            if s + RAW_BUFS < TOTAL:
                load_w1(s + RAW_BUFS)

        z2, negmax2, e2, esum2 = softmax_tiles(1)
        weight2 = small.tile([P, B_TILES], F32)
        result = soft.tile([P, B_TILES, C], F32)
        out_tiles = out.rearrange("(p i) c -> i p c", i=B_TILES)
        last = TOTAL - 1
        parts = batch_parts(last)
        tiles = [slice(*pair) for pair in LAST_ROUND_TILES]
        for k in range(1, len(parts)):
            layer1_passes(last, range(PACK), [k])
            layer1_exits(last, range(PACK), [k])
        regroup_h(last, parts[0])
        fill()
        quantise_h(last - 1, WHOLE)
        fill()
        layer2(last - 1)
        for k in range(len(parts)):
            if k + 1 < len(parts):
                quantise_h(last, parts[k])
                if k == 0:
                    fill()
                layer2(last, range(tiles[k].start, tiles[k].stop))
                regroup_h(last, parts[k + 1])
            else:
                quantise_h(last, parts[k])
                layer2(last, range(tiles[k].start, tiles[k].stop))
            if k == 0:
                fill(len(gate_queue))
                share1 = soft.tile([P, B_TILES, C], F32)
                for i in range(B_TILES):
                    nc.scalar.activation(
                        out=share1[:, i, :], in_=e1[:, i, :], func=ACT.Copy, scale=keep[:, i : i + 1]
                    )
            else:
                for i in range(tiles[k - 1].start, tiles[k - 1].stop):
                    add_b2(1, z2, i)
                if k > 1:
                    row_max(z2, negmax2, tiles[k - 2])
                    for i in range(tiles[k - 2].start, tiles[k - 2].stop):
                        exponential(z2, negmax2, e2, esum2, i)
        row_max(z2, negmax2, tiles[-2])
        for i in range(tiles[-1].start, tiles[-1].stop):
            add_b2(1, z2, i)
        for i in range(tiles[-2].start, tiles[-2].stop):
            exponential(z2, negmax2, e2, esum2, i)
        row_max(z2, negmax2, tiles[-1])
        for i in range(tiles[-1].start, tiles[-1].stop):
            exponential(z2, negmax2, e2, esum2, i)
        for pair in tiles:
            nc.vector.reciprocal(out=weight2[:, pair], in_=esum2[:, pair])
            for i in range(pair.start, pair.stop):
                nc.vector.tensor_scalar_mul(out=z2[:, i, :], in0=e2[:, i, :], scalar1=cond[:, i : i + 1])
            for i in range(pair.start, pair.stop):
                nc.vector.scalar_tensor_tensor(
                    out=result[:, i, :],
                    in0=z2[:, i, :],
                    scalar=weight2[:, i : i + 1],
                    in1=share1[:, i, :],
                    op0=ALU.mult,
                    op1=ALU.add,
                )
                nc.sync.dma_start(out=out_tiles[i], in_=result[:, i, :])
